import numpy as np
import ml_dtypes


def mxq(x, axis, fmt="e4m3"):
    dtype, down = {"e4m3": (ml_dtypes.float8_e4m3fn, 7), "e5m2": (ml_dtypes.float8_e5m2, 14)}[fmt]
    v = np.moveaxis(np.asarray(x, np.float32).astype(ml_dtypes.bfloat16).astype(np.float64), axis, -1)
    blocks = v.reshape(v.shape[:-1] + (-1, 32))
    amax = np.abs(blocks).max(-1, keepdims=True)
    byte = np.maximum(np.where(amax > 0, np.frexp(amax)[1] - 1 + 127, 0) - down, 1)
    scale = np.exp2(byte - 127.0)
    codes = (blocks / scale).astype(np.float32).astype(dtype).astype(np.float64)
    return np.moveaxis((codes * scale).reshape(v.shape), -1, axis)


WIDE = False


def mx_kscale(k):
    if not WIDE:
        return np.ones(k)
    levels = np.array([10, -10, 5, -5, 0])
    if k % 512:
        return np.exp2(np.random.permutation(np.resize(levels, k // 32))).repeat(32)
    a = np.empty((k // 512, 16))
    for p in range(k // 512):
        a[p, :8] = np.random.permutation(np.resize(levels, 8))
        for g in range(8):
            far = levels[np.abs(levels - a[p, g]) >= 10]
            a[p, g + 8] = far[np.random.randint(len(far))]
    return np.exp2(a.ravel()).repeat(32)


BF16 = ml_dtypes.bfloat16


def bf(x):
    return np.asarray(x, np.float32).astype(BF16)


def f64(x):
    return np.asarray(x).astype(np.float64)


B, T, E, H, C, W = 1, 4096, 512, 4, 250, 256
D = E // H
MAX_PERIOD = 10000.0


def rope_tables():
    freqs = np.exp(np.arange(D // 2, dtype=np.float64) * (-np.log(MAX_PERIOD) * 2.0 / D))
    ang = np.arange(T, dtype=np.float64)[:, None] * freqs[None, :]
    return np.cos(ang), np.sin(ang)


def rot(x, cos, sin):
    xr = x.reshape(B, H, T, D // 2, 2)
    xa, xb = xr[..., 0], xr[..., 1]
    ya = xa * cos - xb * sin
    yb = xa * sin + xb * cos
    return np.stack([ya, yb], axis=-1).reshape(B, H, T, D)


def setup_inputs():
    s = mx_kscale(E)
    return {"query": bf(np.random.standard_normal((B, T, E)) * s),
            "in_proj_w": bf(np.random.standard_normal((3 * E, E)) / np.sqrt(E) / s[None, :])}


def reference(query, in_proj_w):
    proj = mxq(f64(query), 2, "e4m3") @ mxq(f64(in_proj_w), 1, "e4m3").T
    qkv = proj.reshape(B, T, 3, H, D)
    q = qkv[:, :, 0].transpose(0, 2, 1, 3)
    k = qkv[:, :, 1].transpose(0, 2, 1, 3)
    v = qkv[:, :, 2].transpose(0, 2, 1, 3)
    cos, sin = rope_tables()
    return rot(q, cos, sin), rot(k, cos, sin), v

@@ -1,0 +1,213 @@
+import math
+from contextlib import ExitStack
+
+import concourse.mybir as mybir
+from concourse.masks import make_identity
+
+F32 = mybir.dt.float32
+BF16 = mybir.dt.bfloat16
+I32 = mybir.dt.int32
+U32 = mybir.dt.uint32
+U8 = mybir.dt.uint8
+FP8X4 = mybir.dt.float8_e4m3fn_x4
+ALU = mybir.AluOpType
+ACT = mybir.ActivationFunctionType
+
+P = 128
+TOKENS = 4096
+EMBED = 512
+HEADS = 4
+HEAD_DIM = 128
+PAIRS = HEAD_DIM // 2
+MAX_PERIOD = 10000.0
+BANK = 512
+BLOCKS = BANK // P
+TILES = TOKENS // P
+CHUNK = BLOCKS
+CHUNKS = TILES // CHUNK
+ROTATED = 2 * HEADS
+ROUND_MAGIC = 12582912.0
+
+FLOPS = 2 * TOKENS * 3 * EMBED * EMBED
+
+
+def tile_mimistreamingmultiheadattention_pa_t_kernel(
+    tc, query, in_proj_w, out_0, out_1, out_2
+):
+    nc = tc.nc
+    with ExitStack() as ctx:
+        keep = ctx.enter_context(tc.tile_pool(name="keep", bufs=1))
+        work = ctx.enter_context(tc.tile_pool(name="work", bufs=2))
+        psum = ctx.enter_context(tc.psum_pool(name="psum", bufs=2))
+
+        tokens = query.rearrange("b (p i) e -> p (b i) e", i=TILES)
+        pair_rows = in_proj_w[0 : 2 * EMBED, :].rearrange("(m r e) k -> e r m k", r=P, e=2)
+        v_rows = in_proj_w[2 * EMBED : 3 * EMBED, :].rearrange("(m r) k -> r m k", r=P)
+
+        x_raw = []
+        for c in range(CHUNKS):
+            x_raw.append(keep.tile([P, CHUNK, EMBED], BF16, name="x_raw%d" % c))
+        w_raw = {}
+        for part in ("first", "second", "v"):
+            w_raw[part] = keep.tile([P, BLOCKS, EMBED], BF16, name="w_raw_" + part)
+
+        nc.sync.dma_start(out=w_raw["second"][:], in_=pair_rows[1])
+        nc.sync.dma_start(out=w_raw["first"][:], in_=pair_rows[0])
+        nc.sync.dma_start(out=x_raw[0][:], in_=tokens[:, 0:CHUNK, :])
+        nc.sync.dma_start(out=w_raw["v"][:], in_=v_rows)
+        for c in range(1, CHUNKS):
+            nc.sync.dma_start(out=x_raw[c][:], in_=tokens[:, c * CHUNK : (c + 1) * CHUNK, :])
+
+        identity = keep.tile([P, P], F32, name="identity")
+        make_identity(nc, identity[:])
+
+        position_int = keep.tile([P, TILES], I32, name="position_int")
+        nc.gpsimd.iota(out=position_int[:], pattern=[[1, TILES]], base=0, channel_multiplier=TILES)
+        position = keep.tile([P, TILES], F32, name="position")
+        nc.vector.tensor_copy(out=position[:], in_=position_int[:])
+
+        magic = keep.tile([P, 1], F32, name="magic")
+        nc.vector.memset(magic[:], ROUND_MAGIC)
+        plus_eighth = keep.tile([P, 1], F32, name="plus_eighth")
+        nc.vector.memset(plus_eighth[:], 0.125)
+        minus_eighth = keep.tile([P, 1], F32, name="minus_eighth")
+        nc.vector.memset(minus_eighth[:], -0.125)
+        one = keep.tile([P, 1], F32, name="one")
+        nc.vector.memset(one[:], 1.0)
+
+        turns_per_token = keep.tile([P, PAIRS], F32, name="turns_per_token")
+        nc.vector.tensor_scalar(
+            out=turns_per_token[:, 0:1], in0=one[:], scalar1=1.0 / (2.0 * math.pi), scalar2=None, op0=ALU.mult
+        )
+        ratio = MAX_PERIOD ** (-1.0 / PAIRS)
+        for m in (1, 2, 4, 8, 16, 32):
+            nc.vector.tensor_scalar(
+                out=turns_per_token[:, m : 2 * m],
+                in0=turns_per_token[:, 0:m],
+                scalar1=ratio**m,
+                scalar2=None,
+                op0=ALU.mult,
+            )
+
+        def quantise_rows(raw, name, bufs, copy_out):
+            grouped = work.tile([P, 4 * BANK], BF16, name="grouped", align_bytes=64)
+            words = grouped[:].bitcast(F32).rearrange("p (c u) -> p c u", u=2)
+            for half in range(2):
+                flipped = psum.tile([P, 2, 2 * P], F32, name="flipped")
+                for b in range(2):
+                    block = raw[:, 2 * half + b, :].bitcast(F32)
+                    for u in range(2):
+                        nc.tensor.transpose(
+                            out=flipped[:, u, b * P : (b + 1) * P],
+                            in_=block[:, u : 2 * P : 2],
+                            identity=identity[:],
+                        )
+                copy_out(
+                    out=words[:, half * 2 * P : (half + 1) * 2 * P, :],
+                    in_=flipped[:].rearrange("p u c -> p c u"),
+                )
+            codes = work.tile([P, BANK], U32, name=name + "_codes", bufs=bufs, align_bytes=64)
+            scales = work.tile([P, BANK], U8, name=name + "_scales", bufs=bufs, align_bytes=64)
+            nc.vector.quantize_mx(out=codes[:].bitcast(FP8X4), scales=scales[:], in_=grouped[:])
+            return codes, scales
+
+        def cosine_tables(c):
+            turns = work.tile([P, CHUNK, PAIRS], F32, name="turns")
+            for il in range(CHUNK):
+                i = c * CHUNK + il
+                nc.scalar.activation(
+                    out=turns[:, il, :], in_=turns_per_token[:], func=ACT.Copy, scale=position[:, i : i + 1]
+                )
+            lifted = work.tile([P, CHUNK, PAIRS], F32, name="lifted")
+            nc.scalar.activation(out=lifted[:], in_=turns[:], func=ACT.Identity, bias=magic[:, 0:1], scale=1.0)
+            behind = work.tile([P, CHUNK, PAIRS], F32, name="behind")
+            nc.vector.scalar_tensor_tensor(
+                out=behind[:], in0=lifted[:], scalar=ROUND_MAGIC, in1=turns[:], op0=ALU.subtract, op1=ALU.subtract
+            )
+            distance = work.tile([P, 3, CHUNK, PAIRS], F32, name="distance")
+            nc.scalar.activation(out=distance[:, 0], in_=behind[:], func=ACT.Abs)
+            nc.scalar.activation(out=distance[:, 1], in_=behind[:], func=ACT.Abs, bias=plus_eighth[:, 0:1])
+            nc.scalar.activation(out=distance[:, 2], in_=behind[:], func=ACT.Abs, bias=minus_eighth[:, 0:1])
+            folded = work.tile([P, 3, CHUNK, PAIRS], F32, name="folded")
+            nc.scalar.activation(out=folded[:], in_=distance[:], func=ACT.Copy, scale=-1.0, bias=0.25)
+            cosines = work.tile([P, 3, CHUNK, PAIRS], F32, name="cosines", bufs=3)
+            nc.scalar.activation(out=cosines[:], in_=folded[:], func=ACT.Sin, scale=2.0 * math.pi)
+            return cosines
+
+        def over_heads(table):
+            return table.unsqueeze(1).to_broadcast([P, ROTATED, PAIRS])
+
+        def by_head(columns):
+            return columns.rearrange("p (g j) -> p g j", g=ROTATED)
+
+        weights = {}
+        for part in ("second", "first", "v"):
+            weights[part] = quantise_rows(w_raw[part], "w_" + part, 1, nc.vector.tensor_copy)
+
+        def multiply(bank, x_codes, x_scales, il, part, start, stop):
+            w_codes, w_scales = weights[part]
+            nc.tensor.matmul_mx(
+                out=bank[:],
+                lhsT=x_codes[:, il * P : (il + 1) * P].bitcast(FP8X4),
+                lhsT_scale=x_scales[:, il * P : (il + 1) * P],
+                rhs=w_codes[:].bitcast(FP8X4),
+                rhs_scale=w_scales[:],
+                start=start,
+                stop=stop,
+            )
+
+        stores = (
+            out_0.rearrange("b h (p i) d -> p (b h) i d", i=TILES),
+            out_1.rearrange("b h (p i) d -> p (b h) i d", i=TILES),
+            out_2.rearrange("b h (p i) d -> p (b h) i d", i=TILES),
+        )
+
+        def project_and_rotate(c, x_codes, x_scales, cosines):
+            y_qk = work.tile([P, ROTATED, CHUNK, HEAD_DIM], F32, name="y_qk", bufs=3)
+            y_v = work.tile([P, HEADS, CHUNK, HEAD_DIM], F32, name="y_v", bufs=3)
+            for il in range(CHUNK):
+                second = psum.tile([P, BANK], F32, name="second", tag="acc", bufs=4)
+                multiply(second, x_codes, x_scales, il, "second", True, True)
+                first = psum.tile([P, BANK], F32, name="first", tag="acc", bufs=4)
+                multiply(first, x_codes, x_scales, il, "first", True, True)
+                both = psum.tile([P, BANK], F32, name="both", tag="acc", bufs=4)
+                multiply(both, x_codes, x_scales, il, "first", True, False)
+                multiply(both, x_codes, x_scales, il, "second", False, True)
+                v_bank = psum.tile([P, BANK], F32, name="v_bank")
+                multiply(v_bank, x_codes, x_scales, il, "v", True, True)
+
+                own = work.tile([P, 2, BANK], F32, name="own", bufs=4)
+                nc.vector.scalar_tensor_tensor(
+                    out=by_head(own[:, 0, :]), in0=by_head(second[:]), scalar=-math.sqrt(2.0),
+                    in1=over_heads(cosines[:, 1, il, :]), op0=ALU.mult, op1=ALU.mult,
+                )
+                nc.vector.scalar_tensor_tensor(
+                    out=by_head(own[:, 1, :]), in0=by_head(first[:]), scalar=-math.sqrt(2.0),
+                    in1=over_heads(cosines[:, 2, il, :]), op0=ALU.mult, op1=ALU.mult,
+                )
+                shared = work.tile([P, BANK], F32, name="shared", bufs=4)
+                nc.vector.tensor_tensor(
+                    out=by_head(shared[:]), in0=by_head(both[:]), in1=over_heads(cosines[:, 0, il, :]), op=ALU.mult
+                )
+                adder = nc.vector if il == CHUNK - 1 else nc.gpsimd
+                adder.tensor_tensor(
+                    out=y_qk[:, :, il, :].rearrange("p g (j e) -> p g j e", e=2),
+                    in0=own[:].rearrange("p e (g j) -> p g j e", g=ROTATED),
+                    in1=by_head(shared[:]).unsqueeze(3).to_broadcast([P, ROTATED, PAIRS, 2]),
+                    op=ALU.add,
+                )
+                nc.scalar.copy(out=y_v[:, :, il, :], in_=v_bank[:].rearrange("p (h d) -> p h d", h=HEADS))
+            here = slice(c * CHUNK, (c + 1) * CHUNK)
+            nc.sync.dma_start(out=stores[2][:, :, here, :], in_=y_v[:])
+            nc.sync.dma_start(out=stores[0][:, :, here, :], in_=y_qk[:, 0:HEADS, :, :])
+            nc.sync.dma_start(out=stores[1][:, :, here, :], in_=y_qk[:, HEADS:ROTATED, :, :])
+
+        def prepare(c):
+            x_codes, x_scales = quantise_rows(x_raw[c], "x", 3, nc.scalar.copy)
+            return x_codes, x_scales, cosine_tables(c)
+
+        ready = prepare(0)
+        for c in range(CHUNKS):
+            following = prepare(c + 1) if c + 1 < CHUNKS else None
+            project_and_rotate(c, ready[0], ready[1], ready[2])
+            ready = following

@@ -38,7 +38,8 @@ def tile_mimistreamingmultiheadattention_pa_t_kernel(
     with ExitStack() as ctx:
         keep = ctx.enter_context(tc.tile_pool(name="keep", bufs=1))
         work = ctx.enter_context(tc.tile_pool(name="work", bufs=2))
-        psum = ctx.enter_context(tc.psum_pool(name="psum", bufs=2))
+        psum = ctx.enter_context(tc.psum_pool(name="psum", bufs=8))
+        ctx.enter_context(tc.manual_schedule())
 
         tokens = query.rearrange("b (p i) e -> p (b i) e", i=TILES)
         pair_rows = in_proj_w[0 : 2 * EMBED, :].rearrange("(m r e) k -> e r m k", r=P, e=2)
@@ -52,28 +53,27 @@ def tile_mimistreamingmultiheadattention_pa_t_kernel(
             w_raw[part] = keep.tile([P, BLOCKS, EMBED], BF16, name="w_raw_" + part)
 
         nc.sync.dma_start(out=w_raw["second"][:], in_=pair_rows[1])
-        nc.sync.dma_start(out=w_raw["first"][:], in_=pair_rows[0])
         nc.sync.dma_start(out=x_raw[0][:], in_=tokens[:, 0:CHUNK, :])
+        nc.sync.dma_start(out=w_raw["first"][:], in_=pair_rows[0])
         nc.sync.dma_start(out=w_raw["v"][:], in_=v_rows)
         for c in range(1, CHUNKS):
             nc.sync.dma_start(out=x_raw[c][:], in_=tokens[:, c * CHUNK : (c + 1) * CHUNK, :])
 
-        identity = keep.tile([P, P], F32, name="identity")
-        make_identity(nc, identity[:])
-
-        position_int = keep.tile([P, TILES], I32, name="position_int")
-        nc.gpsimd.iota(out=position_int[:], pattern=[[1, TILES]], base=0, channel_multiplier=TILES)
-        position = keep.tile([P, TILES], F32, name="position")
-        nc.vector.tensor_copy(out=position[:], in_=position_int[:])
-
+        one = keep.tile([P, 1], F32, name="one")
+        nc.vector.memset(one[:], 1.0)
+        warm = keep.tile([P, 1], F32, name="warm")
+        nc.scalar.activation(out=warm[:], in_=one[:], func=ACT.Sin)
         magic = keep.tile([P, 1], F32, name="magic")
         nc.vector.memset(magic[:], ROUND_MAGIC)
         plus_eighth = keep.tile([P, 1], F32, name="plus_eighth")
         nc.vector.memset(plus_eighth[:], 0.125)
         minus_eighth = keep.tile([P, 1], F32, name="minus_eighth")
         nc.vector.memset(minus_eighth[:], -0.125)
-        one = keep.tile([P, 1], F32, name="one")
-        nc.vector.memset(one[:], 1.0)
+
+        position_int = keep.tile([P, TILES], I32, name="position_int")
+        nc.gpsimd.iota(out=position_int[:], pattern=[[1, TILES]], base=0, channel_multiplier=TILES)
+        identity = keep.tile([P, P], F32, name="identity")
+        make_identity(nc, identity[:])
 
         turns_per_token = keep.tile([P, PAIRS], F32, name="turns_per_token")
         nc.vector.tensor_scalar(
@@ -88,30 +88,36 @@ def tile_mimistreamingmultiheadattention_pa_t_kernel(
                 scalar2=None,
                 op0=ALU.mult,
             )
+        position = keep.tile([P, TILES], F32, name="position")
+        nc.vector.tensor_copy(out=position[:], in_=position_int[:])
 
-        def quantise_rows(raw, name, bufs, copy_out):
-            grouped = work.tile([P, 4 * BANK], BF16, name="grouped", align_bytes=64)
+        def flip(raw, half):
+            flipped = psum.tile([P, 2, 2 * P], F32, name="flipped", tag="bank")
+            for b in range(2):
+                block = raw[:, 2 * half + b, :].bitcast(F32)
+                for u in range(2):
+                    nc.tensor.transpose(
+                        out=flipped[:, u, b * P : (b + 1) * P], in_=block[:, u : 2 * P : 2], identity=identity[:]
+                    )
+            return flipped
+
+        def regroup(copy_out, grouped, half, flipped):
             words = grouped[:].bitcast(F32).rearrange("p (c u) -> p c u", u=2)
-            for half in range(2):
-                flipped = psum.tile([P, 2, 2 * P], F32, name="flipped")
-                for b in range(2):
-                    block = raw[:, 2 * half + b, :].bitcast(F32)
-                    for u in range(2):
-                        nc.tensor.transpose(
-                            out=flipped[:, u, b * P : (b + 1) * P],
-                            in_=block[:, u : 2 * P : 2],
-                            identity=identity[:],
-                        )
-                copy_out(
-                    out=words[:, half * 2 * P : (half + 1) * 2 * P, :],
-                    in_=flipped[:].rearrange("p u c -> p c u"),
-                )
+            copy_out(
+                out=words[:, half * 2 * P : (half + 1) * 2 * P, :], in_=flipped[:].rearrange("p u c -> p c u")
+            )
+
+        def new_grouped():
+            grouped = work.tile([P, 4 * BANK], BF16, name="grouped", bufs=3, align_bytes=64)
+            return grouped
+
+        def quantise(grouped, name, bufs):
             codes = work.tile([P, BANK], U32, name=name + "_codes", bufs=bufs, align_bytes=64)
             scales = work.tile([P, BANK], U8, name=name + "_scales", bufs=bufs, align_bytes=64)
             nc.vector.quantize_mx(out=codes[:].bitcast(FP8X4), scales=scales[:], in_=grouped[:])
             return codes, scales
 
-        def cosine_tables(c):
+        def reduce_angles(c):
             turns = work.tile([P, CHUNK, PAIRS], F32, name="turns")
             for il in range(CHUNK):
                 i = c * CHUNK + il
@@ -124,6 +130,9 @@ def tile_mimistreamingmultiheadattention_pa_t_kernel(
             nc.vector.scalar_tensor_tensor(
                 out=behind[:], in0=lifted[:], scalar=ROUND_MAGIC, in1=turns[:], op0=ALU.subtract, op1=ALU.subtract
             )
+            return behind
+
+        def cosine_tables(behind):
             distance = work.tile([P, 3, CHUNK, PAIRS], F32, name="distance")
             nc.scalar.activation(out=distance[:, 0], in_=behind[:], func=ACT.Abs)
             nc.scalar.activation(out=distance[:, 1], in_=behind[:], func=ACT.Abs, bias=plus_eighth[:, 0:1])
@@ -141,10 +150,9 @@ def tile_mimistreamingmultiheadattention_pa_t_kernel(
             return columns.rearrange("p (g j) -> p g j", g=ROTATED)
 
         weights = {}
-        for part in ("second", "first", "v"):
-            weights[part] = quantise_rows(w_raw[part], "w_" + part, 1, nc.vector.tensor_copy)
 
-        def multiply(bank, x_codes, x_scales, il, part, start, stop):
+        def multiply(bank, x_operand, il, part, start, stop):
+            x_codes, x_scales = x_operand
             w_codes, w_scales = weights[part]
             nc.tensor.matmul_mx(
                 out=bank[:],
@@ -162,52 +170,82 @@ def tile_mimistreamingmultiheadattention_pa_t_kernel(
             out_2.rearrange("b h (p i) d -> p (b h) i d", i=TILES),
         )
 
-        def project_and_rotate(c, x_codes, x_scales, cosines):
+        def project(x_operand, il, part):
+            bank = psum.tile([P, BANK], F32, name="bank_" + part, tag="bank")
+            multiply(bank, x_operand, il, part, True, True)
+            return bank
+
+        def project_both(x_operand, il):
+            bank = psum.tile([P, BANK], F32, name="bank_both", tag="bank")
+            multiply(bank, x_operand, il, "first", True, False)
+            multiply(bank, x_operand, il, "second", False, True)
+            return bank
+
+        def weigh(out, bank, table):
+            nc.vector.scalar_tensor_tensor(
+                out=by_head(out), in0=by_head(bank[:]), scalar=-math.sqrt(2.0), in1=over_heads(table),
+                op0=ALU.mult, op1=ALU.mult,
+            )
+
+        def rotate(x_operand, il, cosines, own, shared):
+            second = project(x_operand, il, "second")
+            weigh(own[:, 0, :], second, cosines[:, 1, il, :])
+            first = project(x_operand, il, "first")
+            weigh(own[:, 1, :], first, cosines[:, 2, il, :])
+            both = project_both(x_operand, il)
+            nc.vector.tensor_tensor(
+                out=by_head(shared[:]), in0=by_head(both[:]), in1=over_heads(cosines[:, 0, il, :]), op=ALU.mult
+            )
+
+        def add(y, own, shared):
+            nc.gpsimd.tensor_tensor(
+                out=y.rearrange("p g (j e) -> p g j e", e=2),
+                in0=own[:].rearrange("p e (g j) -> p g j e", g=ROTATED),
+                in1=by_head(shared[:]).unsqueeze(3).to_broadcast([P, ROTATED, PAIRS, 2]),
+                op=ALU.add,
+            )
+
+        behind = reduce_angles(0)
+        cosines = cosine_tables(behind)
+        grouped = {}
+        for part, raw in (("second", w_raw["second"]), ("x", x_raw[0]), ("first", w_raw["first"])):
+            grouped[part] = new_grouped()
+            for half, copy_out in ((0, nc.vector.tensor_copy), (1, nc.scalar.copy)):
+                regroup(copy_out, grouped[part], half, flip(raw, half))
+            if part == "x":
+                weights["second"] = quantise(grouped["second"], "w_second", 1)
+            if part == "first":
+                x_now = quantise(grouped["x"], "x", 2)
+        weights["first"] = quantise(grouped["first"], "w_first", 1)
+
+        following = {}
+        for c in range(CHUNKS):
             y_qk = work.tile([P, ROTATED, CHUNK, HEAD_DIM], F32, name="y_qk", bufs=3)
             y_v = work.tile([P, HEADS, CHUNK, HEAD_DIM], F32, name="y_v", bufs=3)
             for il in range(CHUNK):
-                second = psum.tile([P, BANK], F32, name="second", tag="acc", bufs=4)
-                multiply(second, x_codes, x_scales, il, "second", True, True)
-                first = psum.tile([P, BANK], F32, name="first", tag="acc", bufs=4)
-                multiply(first, x_codes, x_scales, il, "first", True, True)
-                both = psum.tile([P, BANK], F32, name="both", tag="acc", bufs=4)
-                multiply(both, x_codes, x_scales, il, "first", True, False)
-                multiply(both, x_codes, x_scales, il, "second", False, True)
-                v_bank = psum.tile([P, BANK], F32, name="v_bank")
-                multiply(v_bank, x_codes, x_scales, il, "v", True, True)
-
                 own = work.tile([P, 2, BANK], F32, name="own", bufs=4)
-                nc.vector.scalar_tensor_tensor(
-                    out=by_head(own[:, 0, :]), in0=by_head(second[:]), scalar=-math.sqrt(2.0),
-                    in1=over_heads(cosines[:, 1, il, :]), op0=ALU.mult, op1=ALU.mult,
-                )
-                nc.vector.scalar_tensor_tensor(
-                    out=by_head(own[:, 1, :]), in0=by_head(first[:]), scalar=-math.sqrt(2.0),
-                    in1=over_heads(cosines[:, 2, il, :]), op0=ALU.mult, op1=ALU.mult,
-                )
                 shared = work.tile([P, BANK], F32, name="shared", bufs=4)
-                nc.vector.tensor_tensor(
-                    out=by_head(shared[:]), in0=by_head(both[:]), in1=over_heads(cosines[:, 0, il, :]), op=ALU.mult
-                )
-                adder = nc.vector if il == CHUNK - 1 else nc.gpsimd
-                adder.tensor_tensor(
-                    out=y_qk[:, :, il, :].rearrange("p g (j e) -> p g j e", e=2),
-                    in0=own[:].rearrange("p e (g j) -> p g j e", g=ROTATED),
-                    in1=by_head(shared[:]).unsqueeze(3).to_broadcast([P, ROTATED, PAIRS, 2]),
-                    op=ALU.add,
-                )
+                rotate(x_now, il, cosines, own, shared)
+                add(y_qk[:, :, il, :], own, shared)
+                if c == 0 and il == 0:
+                    grouped_v = new_grouped()
+                    for half in range(2):
+                        regroup(nc.scalar.copy, grouped_v, half, flip(w_raw["v"], half))
+                    weights["v"] = quantise(grouped_v, "w_v", 1)
+                v_bank = project(x_now, il, "v")
                 nc.scalar.copy(out=y_v[:, :, il, :], in_=v_bank[:].rearrange("p (h d) -> p h d", h=HEADS))
+                if c + 1 < CHUNKS:
+                    if il == 0:
+                        following["grouped"] = new_grouped()
+                        for half in range(2):
+                            regroup(nc.scalar.copy, following["grouped"], half, flip(x_raw[c + 1], half))
+                    if il == 1:
+                        following["x"] = quantise(following["grouped"], "x", 2)
+                        following["behind"] = reduce_angles(c + 1)
+                    if il == 2:
+                        following["cosines"] = cosine_tables(following["behind"])
             here = slice(c * CHUNK, (c + 1) * CHUNK)
             nc.sync.dma_start(out=stores[2][:, :, here, :], in_=y_v[:])
             nc.sync.dma_start(out=stores[0][:, :, here, :], in_=y_qk[:, 0:HEADS, :, :])
             nc.sync.dma_start(out=stores[1][:, :, here, :], in_=y_qk[:, HEADS:ROTATED, :, :])
-
-        def prepare(c):
-            x_codes, x_scales = quantise_rows(x_raw[c], "x", 3, nc.scalar.copy)
-            return x_codes, x_scales, cosine_tables(c)
-
-        ready = prepare(0)
-        for c in range(CHUNKS):
-            following = prepare(c + 1) if c + 1 < CHUNKS else None
-            project_and_rotate(c, ready[0], ready[1], ready[2])
-            ready = following
+            x_now, cosines = following.get("x"), following.get("cosines")

@@ -42,20 +42,19 @@ def tile_mimistreamingmultiheadattention_pa_t_kernel(
         ctx.enter_context(tc.manual_schedule())
 
         tokens = query.rearrange("b (p i) e -> p (b i) e", i=TILES)
-        pair_rows = in_proj_w[0 : 2 * EMBED, :].rearrange("(m r e) k -> e r m k", r=P, e=2)
-        v_rows = in_proj_w[2 * EMBED : 3 * EMBED, :].rearrange("(m r) k -> r m k", r=P)
+        thirds = in_proj_w.rearrange("(c m r) k -> c r m k", c=3, r=P)
 
         x_raw = []
         for c in range(CHUNKS):
             x_raw.append(keep.tile([P, CHUNK, EMBED], BF16, name="x_raw%d" % c))
         w_raw = {}
-        for part in ("first", "second", "v"):
+        for part in ("q", "k", "v"):
             w_raw[part] = keep.tile([P, BLOCKS, EMBED], BF16, name="w_raw_" + part)
 
-        nc.sync.dma_start(out=w_raw["second"][:], in_=pair_rows[1])
+        nc.sync.dma_start(out=w_raw["q"][:], in_=thirds[0])
         nc.sync.dma_start(out=x_raw[0][:], in_=tokens[:, 0:CHUNK, :])
-        nc.sync.dma_start(out=w_raw["first"][:], in_=pair_rows[0])
-        nc.sync.dma_start(out=w_raw["v"][:], in_=v_rows)
+        nc.sync.dma_start(out=w_raw["k"][:], in_=thirds[1])
+        nc.sync.dma_start(out=w_raw["v"][:], in_=thirds[2])
         for c in range(1, CHUNKS):
             nc.sync.dma_start(out=x_raw[c][:], in_=tokens[:, c * CHUNK : (c + 1) * CHUNK, :])
 
@@ -107,8 +106,18 @@ def tile_mimistreamingmultiheadattention_pa_t_kernel(
                 out=words[:, half * 2 * P : (half + 1) * 2 * P, :], in_=flipped[:].rearrange("p u c -> p c u")
             )
 
+        def regroup_swapped(copy_out, grouped, half, flipped):
+            words = grouped[:].bitcast(F32).rearrange("p (j e u) -> p j e u", e=2, u=2)
+            pairs = flipped[:].rearrange("p u (j e) -> p j e u", e=2)
+            copy_out(out=words[:, half * P : (half + 1) * P, :, :], in_=pairs[:, :, ::-1, :])
+
+        def regroup_elements(copy_out, grouped, quarter, flipped, e):
+            words = grouped[:].bitcast(F32).rearrange("p (c u) -> p c u", u=2)
+            pairs = flipped[:].rearrange("p u (j e) -> p j e u", e=2)
+            copy_out(out=words[:, quarter * P : (quarter + 1) * P, :], in_=pairs[:, :, e, :])
+
         def new_grouped():
-            grouped = work.tile([P, 4 * BANK], BF16, name="grouped", bufs=3, align_bytes=64)
+            grouped = work.tile([P, 4 * BANK], BF16, name="grouped", bufs=5, align_bytes=64)
             return grouped
 
         def quantise(grouped, name, bufs):
@@ -139,9 +148,16 @@ def tile_mimistreamingmultiheadattention_pa_t_kernel(
             nc.scalar.activation(out=distance[:, 2], in_=behind[:], func=ACT.Abs, bias=minus_eighth[:, 0:1])
             folded = work.tile([P, 3, CHUNK, PAIRS], F32, name="folded")
             nc.scalar.activation(out=folded[:], in_=distance[:], func=ACT.Copy, scale=-1.0, bias=0.25)
-            cosines = work.tile([P, 3, CHUNK, PAIRS], F32, name="cosines", bufs=3)
-            nc.scalar.activation(out=cosines[:], in_=folded[:], func=ACT.Sin, scale=2.0 * math.pi)
-            return cosines
+            middle = work.tile([P, CHUNK, PAIRS], F32, name="middle", bufs=3)
+            nc.scalar.activation(out=middle[:], in_=folded[:, 0], func=ACT.Sin, scale=2.0 * math.pi)
+            sides = work.tile([P, CHUNK * PAIRS, 2], F32, name="sides", bufs=3)
+            nc.scalar.activation(
+                out=sides[:],
+                in_=folded[:, 1:3].rearrange("p e i j -> p (i j) e"),
+                func=ACT.Sin,
+                scale=2.0 * math.pi,
+            )
+            return middle, sides
 
         def over_heads(table):
             return table.unsqueeze(1).to_broadcast([P, ROTATED, PAIRS])
@@ -181,51 +197,64 @@ def tile_mimistreamingmultiheadattention_pa_t_kernel(
             multiply(bank, x_operand, il, "second", False, True)
             return bank
 
-        def weigh(out, bank, table):
-            nc.vector.scalar_tensor_tensor(
-                out=by_head(out), in0=by_head(bank[:]), scalar=-math.sqrt(2.0), in1=over_heads(table),
-                op0=ALU.mult, op1=ALU.mult,
-            )
-
-        def rotate(x_operand, il, cosines, own, shared):
-            second = project(x_operand, il, "second")
-            weigh(own[:, 0, :], second, cosines[:, 1, il, :])
-            first = project(x_operand, il, "first")
-            weigh(own[:, 1, :], first, cosines[:, 2, il, :])
+        def rotate(x_operand, il, tables, own, shared):
+            middle, sides = tables
+            side = sides[:, il * PAIRS : (il + 1) * PAIRS, :].rearrange("p j e -> p (j e)")
+            for n, part in enumerate(("q", "k")):
+                swapped = project(x_operand, il, part)
+                nc.vector.scalar_tensor_tensor(
+                    out=own[:, n * HEADS : (n + 1) * HEADS, :],
+                    in0=swapped[:].rearrange("p (h d) -> p h d", h=HEADS),
+                    scalar=-math.sqrt(2.0),
+                    in1=side.unsqueeze(1).to_broadcast([P, HEADS, HEAD_DIM]),
+                    op0=ALU.mult,
+                    op1=ALU.mult,
+                )
             both = project_both(x_operand, il)
             nc.vector.tensor_tensor(
-                out=by_head(shared[:]), in0=by_head(both[:]), in1=over_heads(cosines[:, 0, il, :]), op=ALU.mult
+                out=by_head(shared[:]), in0=by_head(both[:]), in1=over_heads(middle[:, il, :]), op=ALU.mult
             )
 
         def add(y, own, shared):
             nc.gpsimd.tensor_tensor(
                 out=y.rearrange("p g (j e) -> p g j e", e=2),
-                in0=own[:].rearrange("p e (g j) -> p g j e", g=ROTATED),
+                in0=own[:].rearrange("p g (j e) -> p g j e", e=2),
                 in1=by_head(shared[:]).unsqueeze(3).to_broadcast([P, ROTATED, PAIRS, 2]),
                 op=ALU.add,
             )
 
         behind = reduce_angles(0)
-        cosines = cosine_tables(behind)
+        tables = cosine_tables(behind)
         grouped = {}
-        for part, raw in (("second", w_raw["second"]), ("x", x_raw[0]), ("first", w_raw["first"])):
+        copies = (nc.vector.tensor_copy, nc.scalar.copy)
+        for part in ("q", "x", "k", "first", "second"):
             grouped[part] = new_grouped()
-            for half, copy_out in ((0, nc.vector.tensor_copy), (1, nc.scalar.copy)):
-                regroup(copy_out, grouped[part], half, flip(raw, half))
-            if part == "x":
-                weights["second"] = quantise(grouped["second"], "w_second", 1)
-            if part == "first":
-                x_now = quantise(grouped["x"], "x", 2)
-        weights["first"] = quantise(grouped["first"], "w_first", 1)
+        banks = {}
+        for half in range(2):
+            banks["q", half] = flip(w_raw["q"], half)
+            regroup_swapped(copies[half], grouped["q"], half, banks["q", half])
+        for half in range(2):
+            regroup(copies[half], grouped["x"], half, flip(x_raw[0], half))
+        weights["q"] = quantise(grouped["q"], "w_q", 1)
+        for half in range(2):
+            banks["k", half] = flip(w_raw["k"], half)
+            regroup_swapped(copies[half], grouped["k"], half, banks["k", half])
+        x_now = quantise(grouped["x"], "x", 2)
+        for n, part in enumerate(("q", "k")):
+            for half in range(2):
+                for e, element in enumerate(("first", "second")):
+                    regroup_elements(copies[half], grouped[element], 2 * n + half, banks[part, half], e)
+        for part in ("k", "first", "second"):
+            weights[part] = quantise(grouped[part], "w_" + part, 1)
 
         following = {}
         for c in range(CHUNKS):
             y_qk = work.tile([P, ROTATED, CHUNK, HEAD_DIM], F32, name="y_qk", bufs=3)
             y_v = work.tile([P, HEADS, CHUNK, HEAD_DIM], F32, name="y_v", bufs=3)
             for il in range(CHUNK):
-                own = work.tile([P, 2, BANK], F32, name="own", bufs=4)
+                own = work.tile([P, ROTATED, HEAD_DIM], F32, name="own", bufs=4)
                 shared = work.tile([P, BANK], F32, name="shared", bufs=4)
-                rotate(x_now, il, cosines, own, shared)
+                rotate(x_now, il, tables, own, shared)
                 add(y_qk[:, :, il, :], own, shared)
                 if c == 0 and il == 0:
                     grouped_v = new_grouped()
@@ -243,9 +272,9 @@ def tile_mimistreamingmultiheadattention_pa_t_kernel(
                         following["x"] = quantise(following["grouped"], "x", 2)
                         following["behind"] = reduce_angles(c + 1)
                     if il == 2:
-                        following["cosines"] = cosine_tables(following["behind"])
+                        following["tables"] = cosine_tables(following["behind"])
             here = slice(c * CHUNK, (c + 1) * CHUNK)
             nc.sync.dma_start(out=stores[2][:, :, here, :], in_=y_v[:])
             nc.sync.dma_start(out=stores[0][:, :, here, :], in_=y_qk[:, 0:HEADS, :, :])
             nc.sync.dma_start(out=stores[1][:, :, here, :], in_=y_qk[:, HEADS:ROTATED, :, :])
-            x_now, cosines = following.get("x"), following.get("cosines")
+            x_now, tables = following.get("x"), following.get("tables")

@@ -25,6 +25,7 @@ BLOCKS = BANK // P
 TILES = TOKENS // P
 CHUNK = BLOCKS
 CHUNKS = TILES // CHUNK
+TURNED = (6, 7)
 ROTATED = 2 * HEADS
 ROUND_MAGIC = 12582912.0
 
@@ -51,44 +52,57 @@ def tile_mimistreamingmultiheadattention_pa_t_kernel(
         for part in ("q", "k", "v"):
             w_raw[part] = keep.tile([P, BLOCKS, EMBED], BF16, name="w_raw_" + part)
 
-        nc.sync.dma_start(out=w_raw["q"][:], in_=thirds[0])
-        nc.sync.dma_start(out=x_raw[0][:], in_=tokens[:, 0:CHUNK, :])
-        nc.sync.dma_start(out=w_raw["k"][:], in_=thirds[1])
-        nc.sync.dma_start(out=w_raw["v"][:], in_=thirds[2])
-        for c in range(1, CHUNKS):
+        def load_x(c):
             nc.sync.dma_start(out=x_raw[c][:], in_=tokens[:, c * CHUNK : (c + 1) * CHUNK, :])
+
+        nc.sync.dma_start(out=w_raw["q"][:], in_=thirds[0])
+        load_x(0)
+        nc.sync.dma_start(out=w_raw["k"][:], in_=thirds[1])
+        load_x(TURNED[0])
+        nc.sync.dma_start(out=w_raw["v"][:], in_=thirds[2])
+        for c in (1, 2, 3, TURNED[1], 4, 5):
+            load_x(c)
 
         one = keep.tile([P, 1], F32, name="one")
         nc.vector.memset(one[:], 1.0)
         warm = keep.tile([P, 1], F32, name="warm")
         nc.scalar.activation(out=warm[:], in_=one[:], func=ACT.Sin)
+        position = keep.tile([P, TILES], F32, name="position")
+        nc.gpsimd.iota(
+            out=position[:], pattern=[[1, TILES]], base=0, channel_multiplier=TILES,
+            allow_small_or_imprecise_dtypes=True,
+        )
+        identity = keep.tile([P, P], F32, name="identity")
+        make_identity(nc, identity[:])
+        places = {}
+        for c in TURNED:
+            places[c] = keep.tile([P, CHUNK, P], F32, name="place%d" % c)
+            nc.gpsimd.iota(
+                out=places[c][:], pattern=[[1, CHUNK], [TILES, P]], base=c * CHUNK, channel_multiplier=0,
+                allow_small_or_imprecise_dtypes=True,
+            )
+
+        turns_per_token = keep.tile([P, 2 * PAIRS], F32, name="turns_per_token")
+        ratio = MAX_PERIOD ** (-1.0 / PAIRS)
+        step = 8
+        for j in range(step):
+            nc.vector.tensor_scalar(
+                out=turns_per_token[:, j : j + 1], in0=one[:], scalar1=ratio**j / (2.0 * math.pi), scalar2=None,
+                op0=ALU.mult,
+            )
         magic = keep.tile([P, 1], F32, name="magic")
         nc.vector.memset(magic[:], ROUND_MAGIC)
         plus_eighth = keep.tile([P, 1], F32, name="plus_eighth")
         nc.vector.memset(plus_eighth[:], 0.125)
         minus_eighth = keep.tile([P, 1], F32, name="minus_eighth")
         nc.vector.memset(minus_eighth[:], -0.125)
-
-        position_int = keep.tile([P, TILES], I32, name="position_int")
-        nc.gpsimd.iota(out=position_int[:], pattern=[[1, TILES]], base=0, channel_multiplier=TILES)
-        identity = keep.tile([P, P], F32, name="identity")
-        make_identity(nc, identity[:])
-
-        turns_per_token = keep.tile([P, PAIRS], F32, name="turns_per_token")
-        nc.vector.tensor_scalar(
-            out=turns_per_token[:, 0:1], in0=one[:], scalar1=1.0 / (2.0 * math.pi), scalar2=None, op0=ALU.mult
-        )
-        ratio = MAX_PERIOD ** (-1.0 / PAIRS)
-        for m in (1, 2, 4, 8, 16, 32):
+        for j in range(step, PAIRS, step):
             nc.vector.tensor_scalar(
-                out=turns_per_token[:, m : 2 * m],
-                in0=turns_per_token[:, 0:m],
-                scalar1=ratio**m,
-                scalar2=None,
+                out=turns_per_token[:, j : j + step], in0=turns_per_token[:, 0:step], scalar1=ratio**j, scalar2=None,
                 op0=ALU.mult,
             )
-        position = keep.tile([P, TILES], F32, name="position")
-        nc.vector.tensor_copy(out=position[:], in_=position_int[:])
+
+        nc.vector.tensor_copy(out=turns_per_token[:, PAIRS : 2 * PAIRS], in_=turns_per_token[:, 0:PAIRS])
 
         def flip(raw, half):
             flipped = psum.tile([P, 2, 2 * P], F32, name="flipped", tag="bank")
@@ -126,59 +140,155 @@ def tile_mimistreamingmultiheadattention_pa_t_kernel(
             nc.vector.quantize_mx(out=codes[:].bitcast(FP8X4), scales=scales[:], in_=grouped[:])
             return codes, scales
 
-        def reduce_angles(c):
-            turns = work.tile([P, CHUNK, PAIRS], F32, name="turns")
-            for il in range(CHUNK):
-                i = c * CHUNK + il
-                nc.scalar.activation(
-                    out=turns[:, il, :], in_=turns_per_token[:], func=ACT.Copy, scale=position[:, i : i + 1]
-                )
-            lifted = work.tile([P, CHUNK, PAIRS], F32, name="lifted")
+        def lift_angles(c):
+            if c in TURNED:
+                place = places[c][:].rearrange("p i q -> p (i q)")
+                turns = work.tile([P, BANK], F32, name="turns_t", bufs=1)
+                nc.scalar.activation(out=turns[:], in_=place, func=ACT.Copy, scale=turns_of_partition[:, 0:1])
+                lifted = work.tile([P, BANK], F32, name="lifted_t", bufs=1)
+            else:
+                turns = work.tile([P, CHUNK * PAIRS], F32, name="turns", bufs=1)
+                for il in range(CHUNK):
+                    i = c * CHUNK + il
+                    nc.scalar.activation(
+                        out=turns[:, il * PAIRS : (il + 1) * PAIRS], in_=turns_per_token[:, 0:PAIRS], func=ACT.Copy,
+                        scale=position[:, i : i + 1],
+                    )
+                lifted = work.tile([P, CHUNK * PAIRS], F32, name="lifted", bufs=1)
             nc.scalar.activation(out=lifted[:], in_=turns[:], func=ACT.Identity, bias=magic[:, 0:1], scale=1.0)
-            behind = work.tile([P, CHUNK, PAIRS], F32, name="behind")
+            return turns, lifted
+
+        def reduce_angles(c, turns, lifted):
+            behind = lifted if c in TURNED else work.tile([P, CHUNK * PAIRS], F32, name="behind")
             nc.vector.scalar_tensor_tensor(
                 out=behind[:], in0=lifted[:], scalar=ROUND_MAGIC, in1=turns[:], op0=ALU.subtract, op1=ALU.subtract
             )
             return behind
 
-        def cosine_tables(behind):
-            distance = work.tile([P, 3, CHUNK, PAIRS], F32, name="distance")
-            nc.scalar.activation(out=distance[:, 0], in_=behind[:], func=ACT.Abs)
-            nc.scalar.activation(out=distance[:, 1], in_=behind[:], func=ACT.Abs, bias=plus_eighth[:, 0:1])
-            nc.scalar.activation(out=distance[:, 2], in_=behind[:], func=ACT.Abs, bias=minus_eighth[:, 0:1])
-            folded = work.tile([P, 3, CHUNK, PAIRS], F32, name="folded")
-            nc.scalar.activation(out=folded[:], in_=distance[:], func=ACT.Copy, scale=-1.0, bias=0.25)
-            middle = work.tile([P, CHUNK, PAIRS], F32, name="middle", bufs=3)
-            nc.scalar.activation(out=middle[:], in_=folded[:, 0], func=ACT.Sin, scale=2.0 * math.pi)
+        def cosine_tables(c, behind):
+            if c in TURNED:
+                distance = work.tile([P, 3, BANK], F32, name="cosines_t", bufs=1)
+            else:
+                distance = work.tile([P, 3, CHUNK * PAIRS], F32, name="distance", bufs=1)
+            for n, shift in ((1, plus_eighth[:, 0:1]), (2, minus_eighth[:, 0:1]), (0, 0.0)):
+                nc.scalar.activation(out=distance[:, n], in_=behind[:], func=ACT.Abs, bias=shift)
+                if c in TURNED:
+                    sine(distance[:, n], distance[:, n])
+            if c in TURNED:
+                return distance
+            middle = work.tile([P, CHUNK * PAIRS], F32, name="middle", bufs=3)
+            sine(middle[:], distance[:, 0])
             sides = work.tile([P, CHUNK * PAIRS, 2], F32, name="sides", bufs=3)
-            nc.scalar.activation(
-                out=sides[:],
-                in_=folded[:, 1:3].rearrange("p e i j -> p (i j) e"),
-                func=ACT.Sin,
-                scale=2.0 * math.pi,
-            )
+            sine(sides[:], distance[:, 1:3].rearrange("p e c -> p c e"))
             return middle, sides
 
-        def over_heads(table):
-            return table.unsqueeze(1).to_broadcast([P, ROTATED, PAIRS])
+        def sine(table, distance):
+            nc.scalar.activation(out=table, in_=distance, func=ACT.Sin, scale=-2.0 * math.pi, bias=0.5 * math.pi)
+
+        weights = {}
+        operands = {}
+        tables = {}
+        angles = {}
 
         def by_head(columns):
             return columns.rearrange("p (g j) -> p g j", g=ROTATED)
 
-        weights = {}
-
-        def multiply(bank, x_operand, il, part, start, stop):
-            x_codes, x_scales = x_operand
-            w_codes, w_scales = weights[part]
+        def product(bank, still, moving, start, stop):
             nc.tensor.matmul_mx(
-                out=bank[:],
-                lhsT=x_codes[:, il * P : (il + 1) * P].bitcast(FP8X4),
-                lhsT_scale=x_scales[:, il * P : (il + 1) * P],
-                rhs=w_codes[:].bitcast(FP8X4),
-                rhs_scale=w_scales[:],
-                start=start,
-                stop=stop,
+                out=bank[:], lhsT=still[0].bitcast(FP8X4), lhsT_scale=still[1], rhs=moving[0].bitcast(FP8X4),
+                rhs_scale=moving[1], start=start, stop=stop,
             )
+
+        def columns(operand, block):
+            return tuple(part[:, block * P : (block + 1) * P] for part in operand)
+
+        def whole(operand):
+            return tuple(part[:] for part in operand)
+
+        def project(name, factors):
+            bank = psum.tile([P, BANK], F32, name=name, tag="bank")
+            for n, (still, moving) in enumerate(factors):
+                product(bank, still, moving, n == 0, n == len(factors) - 1)
+            return bank
+
+        def weigh(out, bank, table, scalar):
+            if scalar is None:
+                nc.vector.tensor_tensor(out=out, in0=bank, in1=table, op=ALU.mult)
+            else:
+                nc.vector.scalar_tensor_tensor(
+                    out=out, in0=bank, scalar=scalar, in1=table, op0=ALU.mult, op1=ALU.mult
+                )
+
+        minus_root = -math.sqrt(2.0)
+
+        own, shared = {}, {}
+
+        def weigh_own(t, part):
+            c, il = divmod(t, CHUNK)
+            if part == "q":
+                own[t] = work.tile([P, ROTATED, HEAD_DIM], F32, name="own", bufs=4)
+            heads = slice(0, HEADS) if part == "q" else slice(HEADS, ROTATED)
+            side = tables[c][1][:, il * PAIRS : (il + 1) * PAIRS, :].rearrange("p j e -> p (j e)")
+            swapped = project("swapped", [(columns(operands[c], il), whole(weights[part]))])
+            weigh(
+                own[t][:, heads, :],
+                swapped[:].rearrange("p (h d) -> p h d", h=HEADS),
+                side.unsqueeze(1).to_broadcast([P, HEADS, HEAD_DIM]),
+                minus_root,
+            )
+
+        def weigh_shared(t):
+            c, il = divmod(t, CHUNK)
+            shared[t] = work.tile([P, BANK], F32, name="shared", bufs=4)
+            x_tile = columns(operands[c], il)
+            both = project("both", [(x_tile, whole(weights["first"])), (x_tile, whole(weights["second"]))])
+            middle = tables[c][0][:, il * PAIRS : (il + 1) * PAIRS]
+            weigh(by_head(shared[t][:]), by_head(both[:]), middle.unsqueeze(1).to_broadcast([P, ROTATED, PAIRS]), None)
+
+        def add(adder, t, heads, y):
+            count = heads.stop - heads.start
+            adder.tensor_tensor(
+                out=y.rearrange("p g (j e) -> p g j e", e=2),
+                in0=own[t][:, heads, :].rearrange("p g (j e) -> p g j e", e=2),
+                in1=by_head(shared[t][:])[:, heads, :].unsqueeze(3).to_broadcast([P, count, PAIRS, 2]),
+                op=ALU.add,
+            )
+
+        def make_values(c, il, y_v):
+            bank = project("values", [(columns(operands[c], il), whole(weights["v"]))])
+            nc.scalar.copy(out=y_v[:, :, il, :], in_=bank[:].rearrange("p (h d) -> p h d", h=HEADS))
+
+        turned = {}
+
+        def weigh_turned(c, m):
+            turned[c, m] = work.tile([P, 3, BANK], F32, name="turned", bufs=1)
+            moving = whole(operands[c])
+            first, second = columns(weights["first"], m), columns(weights["second"], m)
+            for n, factors, scalar in (
+                (1, [(second, moving)], minus_root),
+                (2, [(first, moving)], minus_root),
+                (0, [(first, moving), (second, moving)], None),
+            ):
+                bank = project("features", factors)
+                weigh(turned[c, m][:, n, :], bank[:], tables[c][:, n, :], scalar)
+
+        def turn(c, m, y):
+            parts = turned[c, m]
+            for pair in range(CHUNK // 2):
+                bank = psum.tile([P, 2, 2, P], F32, name="upright", tag="bank")
+                for i in range(2):
+                    il = 2 * pair + i
+                    for e in range(2):
+                        for n, start in ((1 + e, True), (0, False)):
+                            nc.tensor.matmul(
+                                out=bank[:, i, e, :], lhsT=parts[:, n, il * P : (il + 1) * P], rhs=identity[:],
+                                start=start, stop=not start, is_transpose=True,
+                            )
+                for i in range(2):
+                    nc.scalar.copy(
+                        out=y[:, :, 2 * pair + i, :].rearrange("p h (j e) -> p h j e", e=2),
+                        in_=bank[:, i].rearrange("p e (h j) -> p h j e", h=2),
+                    )
 
         stores = (
             out_0.rearrange("b h (p i) d -> p (b h) i d", i=TILES),
@@ -186,95 +296,158 @@ def tile_mimistreamingmultiheadattention_pa_t_kernel(
             out_2.rearrange("b h (p i) d -> p (b h) i d", i=TILES),
         )
 
-        def project(x_operand, il, part):
-            bank = psum.tile([P, BANK], F32, name="bank_" + part, tag="bank")
-            multiply(bank, x_operand, il, part, True, True)
-            return bank
+        def reduce_and_tabulate(c):
+            tables[c] = cosine_tables(c, reduce_angles(c, *angles[c]))
 
-        def project_both(x_operand, il):
-            bank = psum.tile([P, BANK], F32, name="bank_both", tag="bank")
-            multiply(bank, x_operand, il, "first", True, False)
-            multiply(bank, x_operand, il, "second", False, True)
-            return bank
-
-        def rotate(x_operand, il, tables, own, shared):
-            middle, sides = tables
-            side = sides[:, il * PAIRS : (il + 1) * PAIRS, :].rearrange("p j e -> p (j e)")
-            for n, part in enumerate(("q", "k")):
-                swapped = project(x_operand, il, part)
-                nc.vector.scalar_tensor_tensor(
-                    out=own[:, n * HEADS : (n + 1) * HEADS, :],
-                    in0=swapped[:].rearrange("p (h d) -> p h d", h=HEADS),
-                    scalar=-math.sqrt(2.0),
-                    in1=side.unsqueeze(1).to_broadcast([P, HEADS, HEAD_DIM]),
-                    op0=ALU.mult,
-                    op1=ALU.mult,
-                )
-            both = project_both(x_operand, il)
-            nc.vector.tensor_tensor(
-                out=by_head(shared[:]), in0=by_head(both[:]), in1=over_heads(middle[:, il, :]), op=ALU.mult
-            )
-
-        def add(y, own, shared):
-            nc.gpsimd.tensor_tensor(
-                out=y.rearrange("p g (j e) -> p g j e", e=2),
-                in0=own[:].rearrange("p g (j e) -> p g j e", e=2),
-                in1=by_head(shared[:]).unsqueeze(3).to_broadcast([P, ROTATED, PAIRS, 2]),
-                op=ALU.add,
-            )
-
-        behind = reduce_angles(0)
-        tables = cosine_tables(behind)
+        angles[0] = lift_angles(0)
+        reduce_and_tabulate(0)
+        angles[1] = lift_angles(1)
+        by_vector, by_scalar = nc.vector.tensor_copy, nc.scalar.copy
         grouped = {}
-        copies = (nc.vector.tensor_copy, nc.scalar.copy)
         for part in ("q", "x", "k", "first", "second"):
             grouped[part] = new_grouped()
         banks = {}
         for half in range(2):
             banks["q", half] = flip(w_raw["q"], half)
-            regroup_swapped(copies[half], grouped["q"], half, banks["q", half])
-        for half in range(2):
-            regroup(copies[half], grouped["x"], half, flip(x_raw[0], half))
+            regroup_swapped(by_vector, grouped["q"], half, banks["q", half])
+        spread = psum.tile([P, P], F32, name="spread", tag="bank")
+        nc.tensor.transpose(out=spread[:], in_=turns_per_token[:], identity=identity[:])
+        turns_of_partition = keep.tile([P, 1], F32, name="turns_of_partition")
+        nc.scalar.copy(out=turns_of_partition[:], in_=spread[:, 0:1])
+        for half, copy_out in ((0, by_vector), (1, by_scalar)):
+            regroup(copy_out, grouped["x"], half, flip(x_raw[0], half))
         weights["q"] = quantise(grouped["q"], "w_q", 1)
+        operands[0] = quantise(grouped["x"], "x", 3)
+        behind_1 = reduce_angles(1, *angles[1])
         for half in range(2):
             banks["k", half] = flip(w_raw["k"], half)
-            regroup_swapped(copies[half], grouped["k"], half, banks["k", half])
-        x_now = quantise(grouped["x"], "x", 2)
+            regroup_swapped(by_scalar, grouped["k"], half, banks["k", half])
         for n, part in enumerate(("q", "k")):
             for half in range(2):
+                copy_out = by_vector if (part, half) == ("q", 0) else by_scalar
                 for e, element in enumerate(("first", "second")):
-                    regroup_elements(copies[half], grouped[element], 2 * n + half, banks[part, half], e)
-        for part in ("k", "first", "second"):
+                    regroup_elements(copy_out, grouped[element], 2 * n + half, banks[part, half], e)
+        weights["k"] = quantise(grouped["k"], "w_k", 1)
+        weigh_own(0, "q")
+        weigh_own(0, "k")
+        for part in ("first", "second"):
             weights[part] = quantise(grouped[part], "w_" + part, 1)
 
-        following = {}
-        for c in range(CHUNKS):
-            y_qk = work.tile([P, ROTATED, CHUNK, HEAD_DIM], F32, name="y_qk", bufs=3)
-            y_v = work.tile([P, HEADS, CHUNK, HEAD_DIM], F32, name="y_v", bufs=3)
-            for il in range(CHUNK):
-                own = work.tile([P, ROTATED, HEAD_DIM], F32, name="own", bufs=4)
-                shared = work.tile([P, BANK], F32, name="shared", bufs=4)
-                rotate(x_now, il, tables, own, shared)
-                add(y_qk[:, :, il, :], own, shared)
-                if c == 0 and il == 0:
-                    grouped_v = new_grouped()
-                    for half in range(2):
-                        regroup(nc.scalar.copy, grouped_v, half, flip(w_raw["v"], half))
-                    weights["v"] = quantise(grouped_v, "w_v", 1)
-                v_bank = project(x_now, il, "v")
-                nc.scalar.copy(out=y_v[:, :, il, :], in_=v_bank[:].rearrange("p (h d) -> p h d", h=HEADS))
-                if c + 1 < CHUNKS:
-                    if il == 0:
-                        following["grouped"] = new_grouped()
-                        for half in range(2):
-                            regroup(nc.scalar.copy, following["grouped"], half, flip(x_raw[c + 1], half))
-                    if il == 1:
-                        following["x"] = quantise(following["grouped"], "x", 2)
-                        following["behind"] = reduce_angles(c + 1)
-                    if il == 2:
-                        following["tables"] = cosine_tables(following["behind"])
-            here = slice(c * CHUNK, (c + 1) * CHUNK)
-            nc.sync.dma_start(out=stores[2][:, :, here, :], in_=y_v[:])
-            nc.sync.dma_start(out=stores[0][:, :, here, :], in_=y_qk[:, 0:HEADS, :, :])
-            nc.sync.dma_start(out=stores[1][:, :, here, :], in_=y_qk[:, HEADS:ROTATED, :, :])
-            x_now, tables = following.get("x"), following.get("tables")
+        pending = {}
+
+        def prepare(part):
+            pending[part] = new_grouped()
+            raw = w_raw["v"] if part == "v" else x_raw[part]
+            for half in range(2):
+                regroup(by_scalar, pending[part], half, flip(raw, half))
+
+        def finish(part):
+            if part == "v":
+                weights["v"] = quantise(pending[part], "w_v", 1)
+            elif part in TURNED:
+                operands[part] = quantise(pending[part], "x_t", 2)
+            else:
+                operands[part] = quantise(pending[part], "x", 3)
+
+        LAST = TURNED[0] * CHUNK - 1
+        pieces = [[t, t + 1] for t in range(0, LAST - 1, 2)] + [[LAST - 1], [LAST]]
+        piece_of = {t: piece for piece in pieces for t in piece}
+        y_piece, added, y_values = {}, {}, {}
+
+        def add_heads(adder, t, which):
+            piece = piece_of[t]
+            key = piece[0]
+            if key not in y_piece:
+                count = len(piece)
+                y_piece[key] = work.tile([P, ROTATED, count, HEAD_DIM], F32, name="y_piece", bufs=6)
+            heads = slice(0, ROTATED) if which is None else slice(which * HEADS, (which + 1) * HEADS)
+            add(adder, t, heads, y_piece[key][:, heads, t - key, :])
+            for third in (0, 1) if which is None else (which,):
+                added[key, third] = added.get((key, third), 0) + 1
+                if added[key, third] == len(piece):
+                    nc.sync.dma_start(
+                        out=stores[third][:, :, key : key + len(piece), :],
+                        in_=y_piece[key][:, third * HEADS : (third + 1) * HEADS, :, :],
+                    )
+
+        def make_value(t):
+            c, il = divmod(t, CHUNK)
+            if c not in y_values:
+                y_values[c] = work.tile([P, HEADS, CHUNK, HEAD_DIM], F32, name="y_v", bufs=3)
+            make_values(c, il, y_values[c])
+            if il == CHUNK - 1:
+                nc.scalar.dma_start(out=stores[2][:, :, c * CHUNK : (c + 1) * CHUNK, :], in_=y_values[c][:])
+
+        def turn_and_store(c, m):
+            y_turned = work.tile([P, 2, CHUNK, HEAD_DIM], F32, name="y_turned")
+            turn(c, m, y_turned)
+            heads = slice(2 * (m % 2), 2 * (m % 2) + 2)
+            nc.scalar.dma_start(out=stores[m // 2][:, heads, c * CHUNK : (c + 1) * CHUNK, :], in_=y_turned[:])
+
+        window_quantises = {1: (1,), 2: (2,), 3: (3,), 4: (7,), 5: (4,), 6: (5,)}
+        window_reduces = {1: (2,), 2: (3,), 3: (4,), 4: (7,), 5: (5,)}
+
+        def weigh_both_own(t):
+            weigh_own(t, "q")
+            weigh_own(t, "k")
+
+        angles[6] = lift_angles(6)
+        prepare(6)
+        prepare("v")
+        behind = reduce_angles(6, *angles[6])
+        finish(6)
+        weigh_shared(0)
+        add_heads(nc.gpsimd, 0, None)
+        weigh_both_own(1)
+        weigh_both_own(2)
+        finish("v")
+        tables[6] = cosine_tables(6, behind)
+        weigh_shared(1)
+        add_heads(nc.gpsimd, 1, None)
+        weigh_shared(2)
+        add_heads(nc.gpsimd, 2, 0)
+        weigh_turned(6, 0)
+        for t in range(CHUNK):
+            make_value(t)
+        tables[1] = cosine_tables(1, behind_1)
+        make_value(6 * CHUNK)
+        prepare(1)
+        angles[2] = lift_angles(2)
+
+        for g in range(1, 8):
+            first = 3 * g
+            weigh_both_own(first)
+            add_heads(nc.vector, first - 1, 1)
+            for c in window_quantises.get(g, ()):
+                finish(c)
+            reduced = [(c, reduce_angles(c, *angles[c])) for c in window_reduces.get(g, ())]
+            weigh_shared(first)
+            add_heads(nc.gpsimd, first, None)
+            if first >= CHUNK:
+                make_value(first)
+            for c, behind in reduced:
+                tables[c] = cosine_tables(c, behind)
+            turn_and_store(*divmod(TURNED[0] * CHUNK + g - 1, CHUNK))
+            for c in window_quantises.get(g + 1, ()):
+                prepare(c)
+            weigh_both_own(first + 1)
+            weigh_shared(first + 1)
+            add_heads(nc.gpsimd, first + 1, None)
+            make_value(first + 1)
+            for c in window_reduces.get(g + 1, ()):
+                angles[c] = lift_angles(c)
+            c, m = divmod(TURNED[0] * CHUNK + g, CHUNK)
+            if first + 2 == LAST:
+                weigh_turned(c, m)
+                make_value(c * CHUNK + m)
+            weigh_both_own(first + 2)
+            weigh_shared(first + 2)
+            make_value(first + 2)
+            if first + 2 == LAST:
+                add_heads(nc.vector, LAST, 0)
+                add_heads(nc.vector, LAST, 1)
+                turn_and_store(c, m)
+            else:
+                add_heads(nc.gpsimd, first + 2, 0)
+                weigh_turned(c, m)
+                make_value(c * CHUNK + m)

@@ -58,9 +58,8 @@ def tile_mimistreamingmultiheadattention_pa_t_kernel(
         nc.sync.dma_start(out=w_raw["q"][:], in_=thirds[0])
         load_x(0)
         nc.sync.dma_start(out=w_raw["k"][:], in_=thirds[1])
-        load_x(TURNED[0])
         nc.sync.dma_start(out=w_raw["v"][:], in_=thirds[2])
-        for c in (1, 2, 3, TURNED[1], 4, 5):
+        for c in (TURNED[0], 1, 2, 3, 4, TURNED[1], 5):
             load_x(c)
 
         one = keep.tile([P, 1], F32, name="one")
@@ -156,6 +155,25 @@ def tile_mimistreamingmultiheadattention_pa_t_kernel(
                     )
                 lifted = work.tile([P, CHUNK * PAIRS], F32, name="lifted", bufs=1)
             nc.scalar.activation(out=lifted[:], in_=turns[:], func=ACT.Identity, bias=magic[:, 0:1], scale=1.0)
+            return turns, lifted
+
+        def lift_on_gpsimd(c):
+            size = BANK if c in TURNED else CHUNK * PAIRS
+            turns = work.tile([P, size], F32, name="turns_t" if c in TURNED else "turns", bufs=1)
+            lifted = work.tile([P, size], F32, name="lifted_t" if c in TURNED else "lifted", bufs=1)
+            if c in TURNED:
+                parts = [(slice(0, size), places[c][:].rearrange("p i q -> p (i q)"), turns_of_partition[:, 0:1])]
+            else:
+                parts = [
+                    (slice(il * PAIRS, (il + 1) * PAIRS), turns_per_token[:, 0:PAIRS],
+                     position[:, c * CHUNK + il : c * CHUNK + il + 1])
+                    for il in range(CHUNK)
+                ]
+            for here, step, rate in parts:
+                for out, shift in ((turns, 0.0), (lifted, ROUND_MAGIC)):
+                    nc.gpsimd.tensor_scalar(
+                        out=out[:, here], in0=step, scalar1=rate, scalar2=shift, op0=ALU.mult, op1=ALU.add
+                    )
             return turns, lifted
 
         def reduce_angles(c, turns, lifted):
@@ -301,8 +319,8 @@ def tile_mimistreamingmultiheadattention_pa_t_kernel(
 
         angles[0] = lift_angles(0)
         reduce_and_tabulate(0)
-        angles[1] = lift_angles(1)
         by_vector, by_scalar = nc.vector.tensor_copy, nc.scalar.copy
+        angles[1] = lift_on_gpsimd(1)
         grouped = {}
         for part in ("q", "x", "k", "first", "second"):
             grouped[part] = new_grouped()
@@ -314,11 +332,11 @@ def tile_mimistreamingmultiheadattention_pa_t_kernel(
         nc.tensor.transpose(out=spread[:], in_=turns_per_token[:], identity=identity[:])
         turns_of_partition = keep.tile([P, 1], F32, name="turns_of_partition")
         nc.scalar.copy(out=turns_of_partition[:], in_=spread[:, 0:1])
+        angles[6] = lift_on_gpsimd(6)
         for half, copy_out in ((0, by_vector), (1, by_scalar)):
             regroup(copy_out, grouped["x"], half, flip(x_raw[0], half))
         weights["q"] = quantise(grouped["q"], "w_q", 1)
         operands[0] = quantise(grouped["x"], "x", 3)
-        behind_1 = reduce_angles(1, *angles[1])
         for half in range(2):
             banks["k", half] = flip(w_raw["k"], half)
             regroup_swapped(by_scalar, grouped["k"], half, banks["k", half])
@@ -384,70 +402,80 @@ def tile_mimistreamingmultiheadattention_pa_t_kernel(
             heads = slice(2 * (m % 2), 2 * (m % 2) + 2)
             nc.scalar.dma_start(out=stores[m // 2][:, heads, c * CHUNK : (c + 1) * CHUNK, :], in_=y_turned[:])
 
-        window_quantises = {1: (1,), 2: (2,), 3: (3,), 4: (7,), 5: (4,), 6: (5,)}
+        window_quantises = {1: (6, 2), 2: (3,), 3: (4,), 4: (7,), 5: (5,)}
         window_reduces = {1: (2,), 2: (3,), 3: (4,), 4: (7,), 5: (5,)}
+        values = [c * CHUNK + il for c in (1, 2, 6, 3, 4, 7, 5) for il in range(CHUNK)]
 
         def weigh_both_own(t):
             weigh_own(t, "q")
             weigh_own(t, "k")
 
-        angles[6] = lift_angles(6)
-        prepare(6)
         prepare("v")
-        behind = reduce_angles(6, *angles[6])
-        finish(6)
+        prepare(1)
+        finish("v")
+        behind_1 = reduce_angles(1, *angles[1])
+        behind_6 = reduce_angles(6, *angles[6])
         weigh_shared(0)
         add_heads(nc.gpsimd, 0, None)
+        make_value(0)
+        make_value(1)
         weigh_both_own(1)
+        tables[1] = cosine_tables(1, behind_1)
+        make_value(2)
+        make_value(3)
         weigh_both_own(2)
-        finish("v")
-        tables[6] = cosine_tables(6, behind)
+        finish(1)
         weigh_shared(1)
         add_heads(nc.gpsimd, 1, None)
         weigh_shared(2)
-        add_heads(nc.gpsimd, 2, 0)
-        weigh_turned(6, 0)
-        for t in range(CHUNK):
-            make_value(t)
-        tables[1] = cosine_tables(1, behind_1)
-        make_value(6 * CHUNK)
-        prepare(1)
+        add_heads(nc.gpsimd, 2, None)
+        prepare(6)
+        prepare(2)
+        weigh_both_own(3)
+        weigh_shared(3)
+        add_heads(nc.gpsimd, 3, 0)
         angles[2] = lift_angles(2)
+        tables[6] = cosine_tables(6, behind_6)
 
-        for g in range(1, 8):
-            first = 3 * g
-            weigh_both_own(first)
-            add_heads(nc.vector, first - 1, 1)
-            for c in window_quantises.get(g, ()):
-                finish(c)
-            reduced = [(c, reduce_angles(c, *angles[c])) for c in window_reduces.get(g, ())]
-            weigh_shared(first)
-            add_heads(nc.gpsimd, first, None)
-            if first >= CHUNK:
-                make_value(first)
-            for c, behind in reduced:
-                tables[c] = cosine_tables(c, behind)
-            turn_and_store(*divmod(TURNED[0] * CHUNK + g - 1, CHUNK))
-            for c in window_quantises.get(g + 1, ()):
-                prepare(c)
-            weigh_both_own(first + 1)
-            weigh_shared(first + 1)
-            add_heads(nc.gpsimd, first + 1, None)
-            make_value(first + 1)
-            for c in window_reduces.get(g + 1, ()):
-                angles[c] = lift_angles(c)
-            c, m = divmod(TURNED[0] * CHUNK + g, CHUNK)
-            if first + 2 == LAST:
-                weigh_turned(c, m)
-                make_value(c * CHUNK + m)
-            weigh_both_own(first + 2)
-            weigh_shared(first + 2)
-            make_value(first + 2)
-            if first + 2 == LAST:
-                add_heads(nc.vector, LAST, 0)
-                add_heads(nc.vector, LAST, 1)
-                turn_and_store(c, m)
-            else:
-                add_heads(nc.gpsimd, first + 2, 0)
-                weigh_turned(c, m)
-                make_value(c * CHUNK + m)
+        late = 3
+        groups = [(3 * g + 1, 3 * g + 2, 3 * g + 3) for g in range(1, 7)] + [(LAST - 1,), (LAST,)]
+        for n, group in enumerate(groups):
+            g = n + 1
+            c, m = divmod(TURNED[0] * CHUNK + n, CHUNK)
+            for place, t in enumerate(group):
+                if t == LAST:
+                    weigh_turned(c, m)
+                weigh_both_own(t)
+                if place == 0:
+                    if late is not None:
+                        add_heads(nc.vector, late, 1)
+                        late = None
+                    for part in window_quantises.get(g, ()):
+                        finish(part)
+                    reduced = [(part, reduce_angles(part, *angles[part])) for part in window_reduces.get(g, ())]
+                weigh_shared(t)
+                if place == 0 and g > 1:
+                    turn_and_store(*divmod(TURNED[0] * CHUNK + n - 1, CHUNK))
+                if t == LAST:
+                    add_heads(nc.vector, t, 0)
+                    add_heads(nc.vector, t, 1)
+                elif place == 2:
+                    add_heads(nc.gpsimd, t, 0)
+                    late = t
+                else:
+                    add_heads(nc.gpsimd, t, None)
+                if place == min(1, len(group) - 1) and t != LAST:
+                    weigh_turned(c, m)
+                for t_value in values[5 * (g - 1) + 2 * place : min(5 * (g - 1) + 2 * place + 2, 5 * g)]:
+                    make_value(t_value)
+                if place == 0:
+                    for part, behind in reduced:
+                        tables[part] = cosine_tables(part, behind)
+                if place == min(1, len(group) - 1):
+                    for part in window_quantises.get(g + 1, ()):
+                        prepare(part)
+                if t == LAST:
+                    turn_and_store(c, m)
+                if place == min(1, len(group) - 1):
+                    for part in window_reduces.get(g + 1, ()):
+                        angles[part] = lift_angles(part)

@@ -368,7 +368,7 @@ def tile_mimistreamingmultiheadattention_pa_t_kernel(
                 operands[part] = quantise(pending[part], "x", 3)
 
         LAST = TURNED[0] * CHUNK - 1
-        pieces = [[t, t + 1] for t in range(0, LAST - 1, 2)] + [[LAST - 1], [LAST]]
+        pieces = [[0, 1], [2, 3]] + [list(range(t, t + 4)) for t in range(4, LAST - 4, 4)] + [[LAST - 3, LAST - 2], [LAST - 1], [LAST]]
         piece_of = {t: piece for piece in pieces for t in piece}
         y_piece, added, y_values = {}, {}, {}
 
@@ -377,7 +377,7 @@ def tile_mimistreamingmultiheadattention_pa_t_kernel(
             key = piece[0]
             if key not in y_piece:
                 count = len(piece)
-                y_piece[key] = work.tile([P, ROTATED, count, HEAD_DIM], F32, name="y_piece", bufs=6)
+                y_piece[key] = work.tile([P, ROTATED, count, HEAD_DIM], F32, name="y_piece", bufs=3)
             heads = slice(0, ROTATED) if which is None else slice(which * HEADS, (which + 1) * HEADS)
             add(adder, t, heads, y_piece[key][:, heads, t - key, :])
             for third in (0, 1) if which is None else (which,):

@@ -43,22 +43,23 @@ def tile_mimistreamingmultiheadattention_pa_t_kernel(
         ctx.enter_context(tc.manual_schedule())
 
         tokens = query.rearrange("b (p i) e -> p (b i) e", i=TILES)
-        thirds = in_proj_w.rearrange("(c m r) k -> c r m k", c=3, r=P)
+        pair_rows = in_proj_w[0 : 2 * EMBED, :].rearrange("(m r e) k -> e r m k", r=P, e=2)
+        v_rows = in_proj_w[2 * EMBED : 3 * EMBED, :].rearrange("(m r) k -> r m k", r=P)
 
         x_raw = []
         for c in range(CHUNKS):
             x_raw.append(keep.tile([P, CHUNK, EMBED], BF16, name="x_raw%d" % c))
         w_raw = {}
-        for part in ("q", "k", "v"):
+        for part in ("second", "first", "v"):
             w_raw[part] = keep.tile([P, BLOCKS, EMBED], BF16, name="w_raw_" + part)
 
         def load_x(c):
             nc.sync.dma_start(out=x_raw[c][:], in_=tokens[:, c * CHUNK : (c + 1) * CHUNK, :])
 
-        nc.sync.dma_start(out=w_raw["q"][:], in_=thirds[0])
+        nc.sync.dma_start(out=w_raw["second"][:], in_=pair_rows[1])
         load_x(0)
-        nc.sync.dma_start(out=w_raw["k"][:], in_=thirds[1])
-        nc.sync.dma_start(out=w_raw["v"][:], in_=thirds[2])
+        nc.sync.dma_start(out=w_raw["first"][:], in_=pair_rows[0])
+        nc.sync.dma_start(out=w_raw["v"][:], in_=v_rows)
         for c in (TURNED[0], 1, 2, 3, 4, TURNED[1], 5):
             load_x(c)
 
@@ -118,16 +119,6 @@ def tile_mimistreamingmultiheadattention_pa_t_kernel(
             copy_out(
                 out=words[:, half * 2 * P : (half + 1) * 2 * P, :], in_=flipped[:].rearrange("p u c -> p c u")
             )
-
-        def regroup_swapped(copy_out, grouped, half, flipped):
-            words = grouped[:].bitcast(F32).rearrange("p (j e u) -> p j e u", e=2, u=2)
-            pairs = flipped[:].rearrange("p u (j e) -> p j e u", e=2)
-            copy_out(out=words[:, half * P : (half + 1) * P, :, :], in_=pairs[:, :, ::-1, :])
-
-        def regroup_elements(copy_out, grouped, quarter, flipped, e):
-            words = grouped[:].bitcast(F32).rearrange("p (c u) -> p c u", u=2)
-            pairs = flipped[:].rearrange("p u (j e) -> p j e u", e=2)
-            copy_out(out=words[:, quarter * P : (quarter + 1) * P, :], in_=pairs[:, :, e, :])
 
         def new_grouped():
             grouped = work.tile([P, 4 * BANK], BF16, name="grouped", bufs=5, align_bytes=64)
@@ -196,8 +187,8 @@ def tile_mimistreamingmultiheadattention_pa_t_kernel(
                 return distance
             middle = work.tile([P, CHUNK * PAIRS], F32, name="middle", bufs=3)
             sine(middle[:], distance[:, 0])
-            sides = work.tile([P, CHUNK * PAIRS, 2], F32, name="sides", bufs=3)
-            sine(sides[:], distance[:, 1:3].rearrange("p e c -> p c e"))
+            sides = work.tile([P, 2, CHUNK * PAIRS], F32, name="sides", bufs=3)
+            sine(sides[:], distance[:, 1:3])
             return middle, sides
 
         def sine(table, distance):
@@ -241,19 +232,16 @@ def tile_mimistreamingmultiheadattention_pa_t_kernel(
 
         own, shared = {}, {}
 
-        def weigh_own(t, part):
+        def over_heads(table):
+            return table.unsqueeze(1).to_broadcast([P, ROTATED, PAIRS])
+
+        def weigh_own(t, e):
             c, il = divmod(t, CHUNK)
-            if part == "q":
-                own[t] = work.tile([P, ROTATED, HEAD_DIM], F32, name="own", bufs=4)
-            heads = slice(0, HEADS) if part == "q" else slice(HEADS, ROTATED)
-            side = tables[c][1][:, il * PAIRS : (il + 1) * PAIRS, :].rearrange("p j e -> p (j e)")
-            swapped = project("swapped", [(columns(operands[c], il), whole(weights[part]))])
-            weigh(
-                own[t][:, heads, :],
-                swapped[:].rearrange("p (h d) -> p h d", h=HEADS),
-                side.unsqueeze(1).to_broadcast([P, HEADS, HEAD_DIM]),
-                minus_root,
-            )
+            if e == 0:
+                own[t] = work.tile([P, 2, BANK], F32, name="own", bufs=4)
+            side = tables[c][1][:, e, il * PAIRS : (il + 1) * PAIRS]
+            bank = project("single", [(columns(operands[c], il), whole(weights[("second", "first")[e]]))])
+            weigh(by_head(own[t][:, e, :]), by_head(bank[:]), over_heads(side), minus_root)
 
         def weigh_shared(t):
             c, il = divmod(t, CHUNK)
@@ -261,13 +249,13 @@ def tile_mimistreamingmultiheadattention_pa_t_kernel(
             x_tile = columns(operands[c], il)
             both = project("both", [(x_tile, whole(weights["first"])), (x_tile, whole(weights["second"]))])
             middle = tables[c][0][:, il * PAIRS : (il + 1) * PAIRS]
-            weigh(by_head(shared[t][:]), by_head(both[:]), middle.unsqueeze(1).to_broadcast([P, ROTATED, PAIRS]), None)
+            weigh(by_head(shared[t][:]), by_head(both[:]), over_heads(middle), None)
 
         def add(adder, t, heads, y):
             count = heads.stop - heads.start
             adder.tensor_tensor(
                 out=y.rearrange("p g (j e) -> p g j e", e=2),
-                in0=own[t][:, heads, :].rearrange("p g (j e) -> p g j e", e=2),
+                in0=own[t][:].rearrange("p e (g j) -> p g j e", g=ROTATED)[:, heads, :, :],
                 in1=by_head(shared[t][:])[:, heads, :].unsqueeze(3).to_broadcast([P, count, PAIRS, 2]),
                 op=ALU.add,
             )
@@ -279,7 +267,7 @@ def tile_mimistreamingmultiheadattention_pa_t_kernel(
         turned = {}
 
         def weigh_turned(c, m):
-            turned[c, m] = work.tile([P, 3, BANK], F32, name="turned", bufs=1)
+            turned[c, m] = work.tile([P, 3, BANK], F32, name="turned")
             moving = whole(operands[c])
             first, second = columns(weights["first"], m), columns(weights["second"], m)
             for n, factors, scalar in (
@@ -322,12 +310,10 @@ def tile_mimistreamingmultiheadattention_pa_t_kernel(
         by_vector, by_scalar = nc.vector.tensor_copy, nc.scalar.copy
         angles[1] = lift_on_gpsimd(1)
         grouped = {}
-        for part in ("q", "x", "k", "first", "second"):
+        for part in ("second", "x", "first"):
             grouped[part] = new_grouped()
-        banks = {}
         for half in range(2):
-            banks["q", half] = flip(w_raw["q"], half)
-            regroup_swapped(by_vector, grouped["q"], half, banks["q", half])
+            regroup(by_vector, grouped["second"], half, flip(w_raw["second"], half))
         spread = psum.tile([P, P], F32, name="spread", tag="bank")
         nc.tensor.transpose(out=spread[:], in_=turns_per_token[:], identity=identity[:])
         turns_of_partition = keep.tile([P, 1], F32, name="turns_of_partition")
@@ -335,22 +321,10 @@ def tile_mimistreamingmultiheadattention_pa_t_kernel(
         angles[6] = lift_on_gpsimd(6)
         for half, copy_out in ((0, by_vector), (1, by_scalar)):
             regroup(copy_out, grouped["x"], half, flip(x_raw[0], half))
-        weights["q"] = quantise(grouped["q"], "w_q", 1)
+        weights["second"] = quantise(grouped["second"], "w_second", 1)
         operands[0] = quantise(grouped["x"], "x", 3)
         for half in range(2):
-            banks["k", half] = flip(w_raw["k"], half)
-            regroup_swapped(by_scalar, grouped["k"], half, banks["k", half])
-        for n, part in enumerate(("q", "k")):
-            for half in range(2):
-                copy_out = by_vector if (part, half) == ("q", 0) else by_scalar
-                for e, element in enumerate(("first", "second")):
-                    regroup_elements(copy_out, grouped[element], 2 * n + half, banks[part, half], e)
-        weights["k"] = quantise(grouped["k"], "w_k", 1)
-        weigh_own(0, "q")
-        weigh_own(0, "k")
-        for part in ("first", "second"):
-            weights[part] = quantise(grouped[part], "w_" + part, 1)
-
+            regroup(by_scalar, grouped["first"], half, flip(w_raw["first"], half))
         pending = {}
 
         def prepare(part):
@@ -407,22 +381,25 @@ def tile_mimistreamingmultiheadattention_pa_t_kernel(
         values = [c * CHUNK + il for c in (1, 2, 6, 3, 4, 7, 5) for il in range(CHUNK)]
 
         def weigh_both_own(t):
-            weigh_own(t, "q")
-            weigh_own(t, "k")
+            weigh_own(t, 0)
+            weigh_own(t, 1)
 
         prepare("v")
+        weigh_own(0, 0)
         prepare(1)
+        weights["first"] = quantise(grouped["first"], "w_first", 1)
         finish("v")
         behind_1 = reduce_angles(1, *angles[1])
         behind_6 = reduce_angles(6, *angles[6])
+        weigh_own(0, 1)
         weigh_shared(0)
         add_heads(nc.gpsimd, 0, None)
         make_value(0)
         make_value(1)
         weigh_both_own(1)
-        tables[1] = cosine_tables(1, behind_1)
         make_value(2)
         make_value(3)
+        tables[1] = cosine_tables(1, behind_1)
         weigh_both_own(2)
         finish(1)
         weigh_shared(1)
@@ -454,8 +431,13 @@ def tile_mimistreamingmultiheadattention_pa_t_kernel(
                         finish(part)
                     reduced = [(part, reduce_angles(part, *angles[part])) for part in window_reduces.get(g, ())]
                 weigh_shared(t)
-                if place == 0 and g > 1:
-                    turn_and_store(*divmod(TURNED[0] * CHUNK + n - 1, CHUNK))
+                if len(group) == 1 and t != LAST:
+                    weigh_turned(c, m)
+                if place == 0:
+                    if g > 1:
+                        turn_and_store(*divmod(TURNED[0] * CHUNK + n - 1, CHUNK))
+                    for part in window_quantises.get(g + 1, ()):
+                        prepare(part)
                 if t == LAST:
                     add_heads(nc.vector, t, 0)
                     add_heads(nc.vector, t, 1)
@@ -464,18 +446,19 @@ def tile_mimistreamingmultiheadattention_pa_t_kernel(
                     late = t
                 else:
                     add_heads(nc.gpsimd, t, None)
-                if place == min(1, len(group) - 1) and t != LAST:
+                if place == 1:
                     weigh_turned(c, m)
                 for t_value in values[5 * (g - 1) + 2 * place : min(5 * (g - 1) + 2 * place + 2, 5 * g)]:
                     make_value(t_value)
                 if place == 0:
                     for part, behind in reduced:
-                        tables[part] = cosine_tables(part, behind)
-                if place == min(1, len(group) - 1):
-                    for part in window_quantises.get(g + 1, ()):
-                        prepare(part)
+                        if part not in TURNED:
+                            tables[part] = cosine_tables(part, behind)
                 if t == LAST:
                     turn_and_store(c, m)
                 if place == min(1, len(group) - 1):
+                    for part, behind in reduced:
+                        if part in TURNED:
+                            tables[part] = cosine_tables(part, behind)
                     for part in window_reduces.get(g + 1, ()):
                         angles[part] = lift_angles(part)

@@ -56,8 +56,10 @@ def tile_mimistreamingmultiheadattention_pa_t_kernel(
         def load_x(c):
             nc.sync.dma_start(out=x_raw[c][:], in_=tokens[:, c * CHUNK : (c + 1) * CHUNK, :])
 
-        nc.sync.dma_start(out=w_raw["second"][:], in_=pair_rows[1])
-        load_x(0)
+        for half in (slice(0, 2), slice(2, 4)):
+            nc.sync.dma_start(out=w_raw["second"][:, half, :], in_=pair_rows[1][:, half, :])
+        for half in (slice(0, 2), slice(2, 4)):
+            nc.sync.dma_start(out=x_raw[0][:, half, :], in_=tokens[:, half, :])
         nc.sync.dma_start(out=w_raw["first"][:], in_=pair_rows[0])
         nc.sync.dma_start(out=w_raw["v"][:], in_=v_rows)
         for c in (TURNED[0], 1, 2, 3, 4, TURNED[1], 5):
@@ -264,37 +266,34 @@ def tile_mimistreamingmultiheadattention_pa_t_kernel(
             bank = project("values", [(columns(operands[c], il), whole(weights["v"]))])
             nc.scalar.copy(out=y_v[:, :, il, :], in_=bank[:].rearrange("p (h d) -> p h d", h=HEADS))
 
-        turned = {}
+        turned, y_turned = {}, {}
 
-        def weigh_turned(c, m):
-            turned[c, m] = work.tile([P, 3, BANK], F32, name="turned")
+        def weigh_turned(c, m, n):
+            if n == 1:
+                turned[c, m] = work.tile([P, 3, BANK], F32, name="turned")
             moving = whole(operands[c])
             first, second = columns(weights["first"], m), columns(weights["second"], m)
-            for n, factors, scalar in (
-                (1, [(second, moving)], minus_root),
-                (2, [(first, moving)], minus_root),
-                (0, [(first, moving), (second, moving)], None),
-            ):
-                bank = project("features", factors)
-                weigh(turned[c, m][:, n, :], bank[:], tables[c][:, n, :], scalar)
+            still = ((first, second), (second,), (first,))[n]
+            bank = project("features", [(part, moving) for part in still])
+            weigh(turned[c, m][:, n, :], bank[:], tables[c][:, n, :], minus_root if n else None)
 
-        def turn(c, m, y):
-            parts = turned[c, m]
-            for pair in range(CHUNK // 2):
-                bank = psum.tile([P, 2, 2, P], F32, name="upright", tag="bank")
-                for i in range(2):
-                    il = 2 * pair + i
-                    for e in range(2):
-                        for n, start in ((1 + e, True), (0, False)):
-                            nc.tensor.matmul(
-                                out=bank[:, i, e, :], lhsT=parts[:, n, il * P : (il + 1) * P], rhs=identity[:],
-                                start=start, stop=not start, is_transpose=True,
-                            )
-                for i in range(2):
-                    nc.scalar.copy(
-                        out=y[:, :, 2 * pair + i, :].rearrange("p h (j e) -> p h j e", e=2),
-                        in_=bank[:, i].rearrange("p e (h j) -> p h j e", h=2),
-                    )
+        def turn_half(c, m, half):
+            if half == 0:
+                y_turned[c, m] = work.tile([P, 2, CHUNK, HEAD_DIM], F32, name="y_turned")
+            bank = psum.tile([P, 2, 2, P], F32, name="upright", tag="bank")
+            for i in range(2):
+                here = slice((2 * half + i) * P, (2 * half + i + 1) * P)
+                for e in range(2):
+                    for n, start in ((1 + e, True), (0, False)):
+                        nc.tensor.matmul(
+                            out=bank[:, i, e, :], lhsT=turned[c, m][:, n, here], rhs=identity[:],
+                            start=start, stop=not start, is_transpose=True,
+                        )
+            for i in range(2):
+                nc.scalar.copy(
+                    out=y_turned[c, m][:, :, 2 * half + i, :].rearrange("p h (j e) -> p h j e", e=2),
+                    in_=bank[:, i].rearrange("p e (h j) -> p h j e", h=2),
+                )
 
         stores = (
             out_0.rearrange("b h (p i) d -> p (b h) i d", i=TILES),
@@ -324,14 +323,18 @@ def tile_mimistreamingmultiheadattention_pa_t_kernel(
         weights["second"] = quantise(grouped["second"], "w_second", 1)
         operands[0] = quantise(grouped["x"], "x", 3)
         for half in range(2):
-            regroup(by_scalar, grouped["first"], half, flip(w_raw["first"], half))
+            regroup((by_vector, by_scalar)[half], grouped["first"], half, flip(w_raw["first"], half))
         pending = {}
 
-        def prepare(part):
-            pending[part] = new_grouped()
+        def prepare_half(part, half):
+            if half == 0:
+                pending[part] = new_grouped()
             raw = w_raw["v"] if part == "v" else x_raw[part]
+            regroup(by_scalar, pending[part], half, flip(raw, half))
+
+        def prepare(part):
             for half in range(2):
-                regroup(by_scalar, pending[part], half, flip(raw, half))
+                prepare_half(part, half)
 
         def finish(part):
             if part == "v":
@@ -370,11 +373,9 @@ def tile_mimistreamingmultiheadattention_pa_t_kernel(
             if il == CHUNK - 1:
                 nc.scalar.dma_start(out=stores[2][:, :, c * CHUNK : (c + 1) * CHUNK, :], in_=y_values[c][:])
 
-        def turn_and_store(c, m):
-            y_turned = work.tile([P, 2, CHUNK, HEAD_DIM], F32, name="y_turned")
-            turn(c, m, y_turned)
+        def store_turned(c, m):
             heads = slice(2 * (m % 2), 2 * (m % 2) + 2)
-            nc.scalar.dma_start(out=stores[m // 2][:, heads, c * CHUNK : (c + 1) * CHUNK, :], in_=y_turned[:])
+            nc.scalar.dma_start(out=stores[m // 2][:, heads, c * CHUNK : (c + 1) * CHUNK, :], in_=y_turned[c, m][:])
 
         window_quantises = {1: (6, 2), 2: (3,), 3: (4,), 4: (7,), 5: (5,)}
         window_reduces = {1: (2,), 2: (3,), 3: (4,), 4: (7,), 5: (5,)}
@@ -414,51 +415,77 @@ def tile_mimistreamingmultiheadattention_pa_t_kernel(
         angles[2] = lift_angles(2)
         tables[6] = cosine_tables(6, behind_6)
 
+        def make_some_values(count):
+            for t in values[:count]:
+                make_value(t)
+            values[:] = values[count:]
+
         late = 3
-        groups = [(3 * g + 1, 3 * g + 2, 3 * g + 3) for g in range(1, 7)] + [(LAST - 1,), (LAST,)]
-        for n, group in enumerate(groups):
-            g = n + 1
-            c, m = divmod(TURNED[0] * CHUNK + n, CHUNK)
-            for place, t in enumerate(group):
-                if t == LAST:
-                    weigh_turned(c, m)
-                weigh_both_own(t)
-                if place == 0:
-                    if late is not None:
-                        add_heads(nc.vector, late, 1)
-                        late = None
-                    for part in window_quantises.get(g, ()):
-                        finish(part)
-                    reduced = [(part, reduce_angles(part, *angles[part])) for part in window_reduces.get(g, ())]
-                weigh_shared(t)
-                if len(group) == 1 and t != LAST:
-                    weigh_turned(c, m)
-                if place == 0:
-                    if g > 1:
-                        turn_and_store(*divmod(TURNED[0] * CHUNK + n - 1, CHUNK))
-                    for part in window_quantises.get(g + 1, ()):
-                        prepare(part)
-                if t == LAST:
-                    add_heads(nc.vector, t, 0)
-                    add_heads(nc.vector, t, 1)
-                elif place == 2:
-                    add_heads(nc.gpsimd, t, 0)
-                    late = t
-                else:
-                    add_heads(nc.gpsimd, t, None)
-                if place == 1:
-                    weigh_turned(c, m)
-                for t_value in values[5 * (g - 1) + 2 * place : min(5 * (g - 1) + 2 * place + 2, 5 * g)]:
-                    make_value(t_value)
-                if place == 0:
-                    for part, behind in reduced:
-                        if part not in TURNED:
-                            tables[part] = cosine_tables(part, behind)
-                if t == LAST:
-                    turn_and_store(c, m)
-                if place == min(1, len(group) - 1):
-                    for part, behind in reduced:
-                        if part in TURNED:
-                            tables[part] = cosine_tables(part, behind)
-                    for part in window_reduces.get(g + 1, ()):
-                        angles[part] = lift_angles(part)
+        for g in range(1, 7):
+            first = 3 * g + 1
+            unit = divmod(TURNED[0] * CHUNK + g - 1, CHUNK)
+            unit_before = divmod(TURNED[0] * CHUNK + g - 2, CHUNK)
+            weigh_both_own(first)
+            add_heads(nc.vector, late, 1)
+            for part in window_quantises.get(g, ()):
+                finish(part)
+            reduced = [(part, reduce_angles(part, *angles[part])) for part in window_reduces.get(g, ())]
+            weigh_shared(first)
+            add_heads(nc.gpsimd, first, None)
+            if g > 1:
+                turn_half(*unit_before, 0)
+            weigh_own(first + 1, 0)
+            make_some_values(1)
+            weigh_own(first + 1, 1)
+            if g > 1:
+                turn_half(*unit_before, 1)
+                store_turned(*unit_before)
+            weigh_shared(first + 1)
+            add_heads(nc.gpsimd, first + 1, None)
+            make_some_values(1)
+            for part, behind in reduced:
+                if part not in TURNED:
+                    tables[part] = cosine_tables(part, behind)
+            weigh_turned(*unit, 1)
+            for part in window_quantises.get(g + 1, ()):
+                prepare_half(part, 0)
+            weigh_turned(*unit, 2)
+            make_some_values(1)
+            weigh_turned(*unit, 0)
+            for part in window_quantises.get(g + 1, ()):
+                prepare_half(part, 1)
+            weigh_own(first + 2, 0)
+            make_some_values(1)
+            weigh_own(first + 2, 1)
+            for part in window_reduces.get(g + 1, ()):
+                angles[part] = lift_angles(part)
+            weigh_shared(first + 2)
+            late = first + 2
+            add_heads(nc.gpsimd, late, 0)
+            make_some_values(1)
+            for part, behind in reduced:
+                if part in TURNED:
+                    tables[part] = cosine_tables(part, behind)
+
+        c = TURNED[1]
+        weigh_both_own(LAST - 1)
+        add_heads(nc.vector, late, 1)
+        weigh_shared(LAST - 1)
+        add_heads(nc.gpsimd, LAST - 1, None)
+        for n in (1, 2, 0):
+            weigh_turned(c, 2, n)
+        for half in range(2):
+            turn_half(c, 1, half)
+        store_turned(c, 1)
+        for n in (1, 2, 0):
+            weigh_turned(c, 3, n)
+        weigh_both_own(LAST)
+        weigh_shared(LAST)
+        for half in range(2):
+            turn_half(c, 2, half)
+        store_turned(c, 2)
+        add_heads(nc.vector, LAST, 0)
+        add_heads(nc.vector, LAST, 1)
+        for half in range(2):
+            turn_half(c, 3, half)
+        store_turned(c, 3)

@@ -123,7 +123,7 @@ def tile_mimistreamingmultiheadattention_pa_t_kernel(
             )
 
         def new_grouped():
-            grouped = work.tile([P, 4 * BANK], BF16, name="grouped", bufs=5, align_bytes=64)
+            grouped = work.tile([P, 4 * BANK], BF16, name="grouped", bufs=4, align_bytes=64)
             return grouped
 
         def quantise(grouped, name, bufs):
@@ -279,7 +279,7 @@ def tile_mimistreamingmultiheadattention_pa_t_kernel(
 
         def turn_half(c, m, half):
             if half == 0:
-                y_turned[c, m] = work.tile([P, 2, CHUNK, HEAD_DIM], F32, name="y_turned")
+                y_turned[c, m] = work.tile([P, 2, CHUNK, HEAD_DIM], F32, name="y_turned", bufs=3)
             bank = psum.tile([P, 2, 2, P], F32, name="upright", tag="bank")
             for i in range(2):
                 here = slice((2 * half + i) * P, (2 * half + i + 1) * P)
@@ -420,11 +420,19 @@ def tile_mimistreamingmultiheadattention_pa_t_kernel(
                 make_value(t)
             values[:] = values[count:]
 
+        def transpose_halves(g, half):
+            if g > 1:
+                unit = divmod(TURNED[0] * CHUNK + g - 2, CHUNK)
+                turn_half(*unit, half)
+                if half == 1:
+                    store_turned(*unit)
+            for part in window_quantises.get(g + 1, ()):
+                prepare_half(part, half)
+
         late = 3
         for g in range(1, 7):
             first = 3 * g + 1
             unit = divmod(TURNED[0] * CHUNK + g - 1, CHUNK)
-            unit_before = divmod(TURNED[0] * CHUNK + g - 2, CHUNK)
             weigh_both_own(first)
             add_heads(nc.vector, late, 1)
             for part in window_quantises.get(g, ()):
@@ -432,14 +440,10 @@ def tile_mimistreamingmultiheadattention_pa_t_kernel(
             reduced = [(part, reduce_angles(part, *angles[part])) for part in window_reduces.get(g, ())]
             weigh_shared(first)
             add_heads(nc.gpsimd, first, None)
-            if g > 1:
-                turn_half(*unit_before, 0)
+            transpose_halves(g, 0)
             weigh_own(first + 1, 0)
             make_some_values(1)
             weigh_own(first + 1, 1)
-            if g > 1:
-                turn_half(*unit_before, 1)
-                store_turned(*unit_before)
             weigh_shared(first + 1)
             add_heads(nc.gpsimd, first + 1, None)
             make_some_values(1)
@@ -447,13 +451,10 @@ def tile_mimistreamingmultiheadattention_pa_t_kernel(
                 if part not in TURNED:
                     tables[part] = cosine_tables(part, behind)
             weigh_turned(*unit, 1)
-            for part in window_quantises.get(g + 1, ()):
-                prepare_half(part, 0)
+            transpose_halves(g, 1)
             weigh_turned(*unit, 2)
             make_some_values(1)
             weigh_turned(*unit, 0)
-            for part in window_quantises.get(g + 1, ()):
-                prepare_half(part, 1)
             weigh_own(first + 2, 0)
             make_some_values(1)
             weigh_own(first + 2, 1)

@@ -345,7 +345,7 @@ def tile_mimistreamingmultiheadattention_pa_t_kernel(
                 operands[part] = quantise(pending[part], "x", 3)
 
         LAST = TURNED[0] * CHUNK - 1
-        pieces = [[0, 1], [2, 3]] + [list(range(t, t + 4)) for t in range(4, LAST - 4, 4)] + [[LAST - 3, LAST - 2], [LAST - 1], [LAST]]
+        pieces = [[0, 1], [2, 3]] + [[t, t + 1, t + 2] for t in range(4, LAST - 1, 3)] + [[LAST - 1], [LAST]]
         piece_of = {t: piece for piece in pieces for t in piece}
         y_piece, added, y_values = {}, {}, {}
 
@@ -354,7 +354,7 @@ def tile_mimistreamingmultiheadattention_pa_t_kernel(
             key = piece[0]
             if key not in y_piece:
                 count = len(piece)
-                y_piece[key] = work.tile([P, ROTATED, count, HEAD_DIM], F32, name="y_piece", bufs=3)
+                y_piece[key] = work.tile([P, ROTATED, count, HEAD_DIM], F32, name="y_piece", bufs=4)
             heads = slice(0, ROTATED) if which is None else slice(which * HEADS, (which + 1) * HEADS)
             add(adder, t, heads, y_piece[key][:, heads, t - key, :])
             for third in (0, 1) if which is None else (which,):
@@ -411,7 +411,6 @@ def tile_mimistreamingmultiheadattention_pa_t_kernel(
         prepare(2)
         weigh_both_own(3)
         weigh_shared(3)
-        add_heads(nc.gpsimd, 3, 0)
         angles[2] = lift_angles(2)
         tables[6] = cosine_tables(6, behind_6)
 
@@ -434,7 +433,7 @@ def tile_mimistreamingmultiheadattention_pa_t_kernel(
             first = 3 * g + 1
             unit = divmod(TURNED[0] * CHUNK + g - 1, CHUNK)
             weigh_both_own(first)
-            add_heads(nc.vector, late, 1)
+            add_heads(nc.vector, late, None)
             for part in window_quantises.get(g, ()):
                 finish(part)
             reduced = [(part, reduce_angles(part, *angles[part])) for part in window_reduces.get(g, ())]
@@ -462,7 +461,6 @@ def tile_mimistreamingmultiheadattention_pa_t_kernel(
                 angles[part] = lift_angles(part)
             weigh_shared(first + 2)
             late = first + 2
-            add_heads(nc.gpsimd, late, 0)
             make_some_values(1)
             for part, behind in reduced:
                 if part in TURNED:
@@ -470,7 +468,7 @@ def tile_mimistreamingmultiheadattention_pa_t_kernel(
 
         c = TURNED[1]
         weigh_both_own(LAST - 1)
-        add_heads(nc.vector, late, 1)
+        add_heads(nc.vector, late, None)
         weigh_shared(LAST - 1)
         add_heads(nc.gpsimd, LAST - 1, None)
         for n in (1, 2, 0):

import math
from contextlib import ExitStack

import concourse.mybir as mybir
from concourse.masks import make_identity

F32 = mybir.dt.float32
BF16 = mybir.dt.bfloat16
I32 = mybir.dt.int32
U32 = mybir.dt.uint32
U8 = mybir.dt.uint8
FP8X4 = mybir.dt.float8_e4m3fn_x4
ALU = mybir.AluOpType
ACT = mybir.ActivationFunctionType

P = 128
TOKENS = 4096
EMBED = 512
HEADS = 4
HEAD_DIM = 128
PAIRS = HEAD_DIM // 2
MAX_PERIOD = 10000.0
BANK = 512
BLOCKS = BANK // P
TILES = TOKENS // P
CHUNK = BLOCKS
CHUNKS = TILES // CHUNK
TURNED = (6, 7)
ROTATED = 2 * HEADS
ROUND_MAGIC = 12582912.0

FLOPS = 2 * TOKENS * 3 * EMBED * EMBED


def tile_mimistreamingmultiheadattention_pa_t_kernel(
    tc, query, in_proj_w, out_0, out_1, out_2
):
    nc = tc.nc
    with ExitStack() as ctx:
        keep = ctx.enter_context(tc.tile_pool(name="keep", bufs=1))
        work = ctx.enter_context(tc.tile_pool(name="work", bufs=2))
        psum = ctx.enter_context(tc.psum_pool(name="psum", bufs=8))
        ctx.enter_context(tc.manual_schedule())

        tokens = query.rearrange("b (p i) e -> p (b i) e", i=TILES)
        pair_rows = in_proj_w[0 : 2 * EMBED, :].rearrange("(m r e) k -> e r m k", r=P, e=2)
        v_rows = in_proj_w[2 * EMBED : 3 * EMBED, :].rearrange("(m r) k -> r m k", r=P)

        x_raw = []
        for c in range(CHUNKS):
            x_raw.append(keep.tile([P, CHUNK, EMBED], BF16, name="x_raw%d" % c))
        w_raw = {}
        for part in ("second", "first", "v"):
            w_raw[part] = keep.tile([P, BLOCKS, EMBED], BF16, name="w_raw_" + part)

        def load_x(c):
            nc.sync.dma_start(out=x_raw[c][:], in_=tokens[:, c * CHUNK : (c + 1) * CHUNK, :])

        for half in (slice(0, 2), slice(2, 4)):
            nc.sync.dma_start(out=w_raw["second"][:, half, :], in_=pair_rows[1][:, half, :])
        for half in (slice(0, 2), slice(2, 4)):
            nc.sync.dma_start(out=x_raw[0][:, half, :], in_=tokens[:, half, :])
        nc.sync.dma_start(out=w_raw["first"][:], in_=pair_rows[0])
        nc.sync.dma_start(out=w_raw["v"][:], in_=v_rows)
        for c in (TURNED[0], 1, 2, 3, 4, TURNED[1], 5):
            load_x(c)

        one = keep.tile([P, 1], F32, name="one")
        nc.vector.memset(one[:], 1.0)
        warm = keep.tile([P, 1], F32, name="warm")
        nc.scalar.activation(out=warm[:], in_=one[:], func=ACT.Sin)
        position = keep.tile([P, TILES], F32, name="position")
        nc.gpsimd.iota(
            out=position[:], pattern=[[1, TILES]], base=0, channel_multiplier=TILES,
            allow_small_or_imprecise_dtypes=True,
        )
        identity = keep.tile([P, P], F32, name="identity")
        make_identity(nc, identity[:])
        places = {}
        for c in TURNED:
            places[c] = keep.tile([P, CHUNK, P], F32, name="place%d" % c)
            nc.gpsimd.iota(
                out=places[c][:], pattern=[[1, CHUNK], [TILES, P]], base=c * CHUNK, channel_multiplier=0,
                allow_small_or_imprecise_dtypes=True,
            )

        turns_per_token = keep.tile([P, 2 * PAIRS], F32, name="turns_per_token")
        ratio = MAX_PERIOD ** (-1.0 / PAIRS)
        step = 8
        for j in range(step):
            nc.vector.tensor_scalar(
                out=turns_per_token[:, j : j + 1], in0=one[:], scalar1=ratio**j / (2.0 * math.pi), scalar2=None,
                op0=ALU.mult,
            )
        magic = keep.tile([P, 1], F32, name="magic")
        nc.vector.memset(magic[:], ROUND_MAGIC)
        plus_eighth = keep.tile([P, 1], F32, name="plus_eighth")
        nc.vector.memset(plus_eighth[:], 0.125)
        minus_eighth = keep.tile([P, 1], F32, name="minus_eighth")
        nc.vector.memset(minus_eighth[:], -0.125)
        for j in range(step, PAIRS, step):
            nc.vector.tensor_scalar(
                out=turns_per_token[:, j : j + step], in0=turns_per_token[:, 0:step], scalar1=ratio**j, scalar2=None,
                op0=ALU.mult,
            )

        nc.vector.tensor_copy(out=turns_per_token[:, PAIRS : 2 * PAIRS], in_=turns_per_token[:, 0:PAIRS])

        def flip(raw, half):
            flipped = psum.tile([P, 2, 2 * P], F32, name="flipped", tag="bank")
            for b in range(2):
                block = raw[:, 2 * half + b, :].bitcast(F32)
                for u in range(2):
                    nc.tensor.transpose(
                        out=flipped[:, u, b * P : (b + 1) * P], in_=block[:, u : 2 * P : 2], identity=identity[:]
                    )
            return flipped

        def regroup(copy_out, grouped, half, flipped):
            words = grouped[:].bitcast(F32).rearrange("p (c u) -> p c u", u=2)
            copy_out(
                out=words[:, half * 2 * P : (half + 1) * 2 * P, :], in_=flipped[:].rearrange("p u c -> p c u")
            )

        def new_grouped():
            grouped = work.tile([P, 4 * BANK], BF16, name="grouped", bufs=4, align_bytes=64)
            return grouped

        def quantise(grouped, name, bufs):
            codes = work.tile([P, BANK], U32, name=name + "_codes", bufs=bufs, align_bytes=64)
            scales = work.tile([P, BANK], U8, name=name + "_scales", bufs=bufs, align_bytes=64)
            nc.vector.quantize_mx(out=codes[:].bitcast(FP8X4), scales=scales[:], in_=grouped[:])
            return codes, scales

        def lift_angles(c):
            if c in TURNED:
                place = places[c][:].rearrange("p i q -> p (i q)")
                turns = work.tile([P, BANK], F32, name="turns_t", bufs=1)
                nc.scalar.activation(out=turns[:], in_=place, func=ACT.Copy, scale=turns_of_partition[:, 0:1])
                lifted = work.tile([P, BANK], F32, name="lifted_t", bufs=1)
            else:
                turns = work.tile([P, CHUNK * PAIRS], F32, name="turns", bufs=1)
                for il in range(CHUNK):
                    i = c * CHUNK + il
                    nc.scalar.activation(
                        out=turns[:, il * PAIRS : (il + 1) * PAIRS], in_=turns_per_token[:, 0:PAIRS], func=ACT.Copy,
                        scale=position[:, i : i + 1],
                    )
                lifted = work.tile([P, CHUNK * PAIRS], F32, name="lifted", bufs=1)
            nc.scalar.activation(out=lifted[:], in_=turns[:], func=ACT.Identity, bias=magic[:, 0:1], scale=1.0)
            return turns, lifted

        def lift_on_gpsimd(c):
            size = BANK if c in TURNED else CHUNK * PAIRS
            turns = work.tile([P, size], F32, name="turns_t" if c in TURNED else "turns", bufs=1)
            lifted = work.tile([P, size], F32, name="lifted_t" if c in TURNED else "lifted", bufs=1)
            if c in TURNED:
                parts = [(slice(0, size), places[c][:].rearrange("p i q -> p (i q)"), turns_of_partition[:, 0:1])]
            else:
                parts = [
                    (slice(il * PAIRS, (il + 1) * PAIRS), turns_per_token[:, 0:PAIRS],
                     position[:, c * CHUNK + il : c * CHUNK + il + 1])
                    for il in range(CHUNK)
                ]
            for here, step, rate in parts:
                for out, shift in ((turns, 0.0), (lifted, ROUND_MAGIC)):
                    nc.gpsimd.tensor_scalar(
                        out=out[:, here], in0=step, scalar1=rate, scalar2=shift, op0=ALU.mult, op1=ALU.add
                    )
            return turns, lifted

        def reduce_angles(c, turns, lifted):
            behind = lifted if c in TURNED else work.tile([P, CHUNK * PAIRS], F32, name="behind")
            nc.vector.scalar_tensor_tensor(
                out=behind[:], in0=lifted[:], scalar=ROUND_MAGIC, in1=turns[:], op0=ALU.subtract, op1=ALU.subtract
            )
            return behind

        def cosine_tables(c, behind):
            if c in TURNED:
                distance = work.tile([P, 3, BANK], F32, name="cosines_t", bufs=1)
            else:
                distance = work.tile([P, 3, CHUNK * PAIRS], F32, name="distance", bufs=1)
            for n, shift in ((1, plus_eighth[:, 0:1]), (2, minus_eighth[:, 0:1]), (0, 0.0)):
                nc.scalar.activation(out=distance[:, n], in_=behind[:], func=ACT.Abs, bias=shift)
                if c in TURNED:
                    sine(distance[:, n], distance[:, n])
            if c in TURNED:
                return distance
            middle = work.tile([P, CHUNK * PAIRS], F32, name="middle", bufs=3)
            sine(middle[:], distance[:, 0])
            sides = work.tile([P, 2, CHUNK * PAIRS], F32, name="sides", bufs=3)
            sine(sides[:], distance[:, 1:3])
            return middle, sides

        def sine(table, distance):
            nc.scalar.activation(out=table, in_=distance, func=ACT.Sin, scale=-2.0 * math.pi, bias=0.5 * math.pi)

        weights = {}
        operands = {}
        tables = {}
        angles = {}

        def by_head(columns):
            return columns.rearrange("p (g j) -> p g j", g=ROTATED)

        def product(bank, still, moving, start, stop):
            nc.tensor.matmul_mx(
                out=bank[:], lhsT=still[0].bitcast(FP8X4), lhsT_scale=still[1], rhs=moving[0].bitcast(FP8X4),
                rhs_scale=moving[1], start=start, stop=stop,
            )

        def columns(operand, block):
            return tuple(part[:, block * P : (block + 1) * P] for part in operand)

        def whole(operand):
            return tuple(part[:] for part in operand)

        def project(name, factors):
            bank = psum.tile([P, BANK], F32, name=name, tag="bank")
            for n, (still, moving) in enumerate(factors):
                product(bank, still, moving, n == 0, n == len(factors) - 1)
            return bank

        def weigh(out, bank, table, scalar):
            if scalar is None:
                nc.vector.tensor_tensor(out=out, in0=bank, in1=table, op=ALU.mult)
            else:
                nc.vector.scalar_tensor_tensor(
                    out=out, in0=bank, scalar=scalar, in1=table, op0=ALU.mult, op1=ALU.mult
                )

        minus_root = -math.sqrt(2.0)

        own, shared = {}, {}

        def over_heads(table):
            return table.unsqueeze(1).to_broadcast([P, ROTATED, PAIRS])

        def weigh_own(t, e):
            c, il = divmod(t, CHUNK)
            if e == 0:
                own[t] = work.tile([P, 2, BANK], F32, name="own", bufs=4)
            side = tables[c][1][:, e, il * PAIRS : (il + 1) * PAIRS]
            bank = project("single", [(columns(operands[c], il), whole(weights[("second", "first")[e]]))])
            weigh(by_head(own[t][:, e, :]), by_head(bank[:]), over_heads(side), minus_root)

        def weigh_shared(t):
            c, il = divmod(t, CHUNK)
            shared[t] = work.tile([P, BANK], F32, name="shared", bufs=4)
            x_tile = columns(operands[c], il)
            both = project("both", [(x_tile, whole(weights["first"])), (x_tile, whole(weights["second"]))])
            middle = tables[c][0][:, il * PAIRS : (il + 1) * PAIRS]
            weigh(by_head(shared[t][:]), by_head(both[:]), over_heads(middle), None)

        def add(adder, t, heads, y):
            count = heads.stop - heads.start
            adder.tensor_tensor(
                out=y.rearrange("p g (j e) -> p g j e", e=2),
                in0=own[t][:].rearrange("p e (g j) -> p g j e", g=ROTATED)[:, heads, :, :],
                in1=by_head(shared[t][:])[:, heads, :].unsqueeze(3).to_broadcast([P, count, PAIRS, 2]),
                op=ALU.add,
            )

        def make_values(c, il, y_v):
            bank = project("values", [(columns(operands[c], il), whole(weights["v"]))])
            nc.scalar.copy(out=y_v[:, :, il, :], in_=bank[:].rearrange("p (h d) -> p h d", h=HEADS))

        turned, y_turned = {}, {}

        def weigh_turned(c, m, n):
            if n == 1:
                turned[c, m] = work.tile([P, 3, BANK], F32, name="turned")
            moving = whole(operands[c])
            first, second = columns(weights["first"], m), columns(weights["second"], m)
            still = ((first, second), (second,), (first,))[n]
            bank = project("features", [(part, moving) for part in still])
            weigh(turned[c, m][:, n, :], bank[:], tables[c][:, n, :], minus_root if n else None)

        def turn_half(c, m, half):
            if half == 0:
                y_turned[c, m] = work.tile([P, 2, CHUNK, HEAD_DIM], F32, name="y_turned", bufs=3)
            bank = psum.tile([P, 2, 2, P], F32, name="upright", tag="bank")
            for i in range(2):
                here = slice((2 * half + i) * P, (2 * half + i + 1) * P)
                for e in range(2):
                    for n, start in ((1 + e, True), (0, False)):
                        nc.tensor.matmul(
                            out=bank[:, i, e, :], lhsT=turned[c, m][:, n, here], rhs=identity[:],
                            start=start, stop=not start, is_transpose=True,
                        )
            for i in range(2):
                nc.scalar.copy(
                    out=y_turned[c, m][:, :, 2 * half + i, :].rearrange("p h (j e) -> p h j e", e=2),
                    in_=bank[:, i].rearrange("p e (h j) -> p h j e", h=2),
                )

        stores = (
            out_0.rearrange("b h (p i) d -> p (b h) i d", i=TILES),
            out_1.rearrange("b h (p i) d -> p (b h) i d", i=TILES),
            out_2.rearrange("b h (p i) d -> p (b h) i d", i=TILES),
        )

        def reduce_and_tabulate(c):
            tables[c] = cosine_tables(c, reduce_angles(c, *angles[c]))

        angles[0] = lift_angles(0)
        reduce_and_tabulate(0)
        by_vector, by_scalar = nc.vector.tensor_copy, nc.scalar.copy
        angles[1] = lift_on_gpsimd(1)
        grouped = {}
        for part in ("second", "x", "first"):
            grouped[part] = new_grouped()
        for half in range(2):
            regroup(by_vector, grouped["second"], half, flip(w_raw["second"], half))
        spread = psum.tile([P, P], F32, name="spread", tag="bank")
        nc.tensor.transpose(out=spread[:], in_=turns_per_token[:], identity=identity[:])
        turns_of_partition = keep.tile([P, 1], F32, name="turns_of_partition")
        nc.scalar.copy(out=turns_of_partition[:], in_=spread[:, 0:1])
        angles[6] = lift_on_gpsimd(6)
        for half, copy_out in ((0, by_vector), (1, by_scalar)):
            regroup(copy_out, grouped["x"], half, flip(x_raw[0], half))
        weights["second"] = quantise(grouped["second"], "w_second", 1)
        operands[0] = quantise(grouped["x"], "x", 3)
        for half in range(2):
            regroup((by_vector, by_scalar)[half], grouped["first"], half, flip(w_raw["first"], half))
        pending = {}

        def prepare_half(part, half):
            if half == 0:
                pending[part] = new_grouped()
            raw = w_raw["v"] if part == "v" else x_raw[part]
            regroup(by_scalar, pending[part], half, flip(raw, half))

        def prepare(part):
            for half in range(2):
                prepare_half(part, half)

        def finish(part):
            if part == "v":
                weights["v"] = quantise(pending[part], "w_v", 1)
            elif part in TURNED:
                operands[part] = quantise(pending[part], "x_t", 2)
            else:
                operands[part] = quantise(pending[part], "x", 3)

        LAST = TURNED[0] * CHUNK - 1
        pieces = [[0, 1], [2, 3]] + [[t, t + 1, t + 2] for t in range(4, LAST - 1, 3)] + [[LAST - 1], [LAST]]
        piece_of = {t: piece for piece in pieces for t in piece}
        y_piece, added, y_values = {}, {}, {}

        def add_heads(adder, t, which):
            piece = piece_of[t]
            key = piece[0]
            if key not in y_piece:
                count = len(piece)
                y_piece[key] = work.tile([P, ROTATED, count, HEAD_DIM], F32, name="y_piece", bufs=4)
            heads = slice(0, ROTATED) if which is None else slice(which * HEADS, (which + 1) * HEADS)
            add(adder, t, heads, y_piece[key][:, heads, t - key, :])
            for third in (0, 1) if which is None else (which,):
                added[key, third] = added.get((key, third), 0) + 1
                if added[key, third] == len(piece):
                    nc.sync.dma_start(
                        out=stores[third][:, :, key : key + len(piece), :],
                        in_=y_piece[key][:, third * HEADS : (third + 1) * HEADS, :, :],
                    )

        def make_value(t):
            c, il = divmod(t, CHUNK)
            if c not in y_values:
                y_values[c] = work.tile([P, HEADS, CHUNK, HEAD_DIM], F32, name="y_v", bufs=3)
            make_values(c, il, y_values[c])
            if il == CHUNK - 1:
                nc.scalar.dma_start(out=stores[2][:, :, c * CHUNK : (c + 1) * CHUNK, :], in_=y_values[c][:])

        def store_turned(c, m):
            heads = slice(2 * (m % 2), 2 * (m % 2) + 2)
            nc.scalar.dma_start(out=stores[m // 2][:, heads, c * CHUNK : (c + 1) * CHUNK, :], in_=y_turned[c, m][:])

        window_quantises = {1: (6, 2), 2: (3,), 3: (4,), 4: (7,), 5: (5,)}
        window_reduces = {1: (2,), 2: (3,), 3: (4,), 4: (7,), 5: (5,)}
        values = [c * CHUNK + il for c in (1, 2, 6, 3, 4, 7, 5) for il in range(CHUNK)]

        def weigh_both_own(t):
            weigh_own(t, 0)
            weigh_own(t, 1)

        prepare("v")
        weigh_own(0, 0)
        prepare(1)
        weights["first"] = quantise(grouped["first"], "w_first", 1)
        finish("v")
        behind_1 = reduce_angles(1, *angles[1])
        behind_6 = reduce_angles(6, *angles[6])
        weigh_own(0, 1)
        weigh_shared(0)
        add_heads(nc.gpsimd, 0, None)
        make_value(0)
        make_value(1)
        weigh_both_own(1)
        make_value(2)
        make_value(3)
        tables[1] = cosine_tables(1, behind_1)
        weigh_both_own(2)
        finish(1)
        weigh_shared(1)
        add_heads(nc.gpsimd, 1, None)
        weigh_shared(2)
        add_heads(nc.gpsimd, 2, None)
        prepare(6)
        prepare(2)
        weigh_both_own(3)
        weigh_shared(3)
        angles[2] = lift_angles(2)
        tables[6] = cosine_tables(6, behind_6)

        def make_some_values(count):
            for t in values[:count]:
                make_value(t)
            values[:] = values[count:]

        def transpose_halves(g, half):
            if g > 1:
                unit = divmod(TURNED[0] * CHUNK + g - 2, CHUNK)
                turn_half(*unit, half)
                if half == 1:
                    store_turned(*unit)
            for part in window_quantises.get(g + 1, ()):
                prepare_half(part, half)

        late = 3
        for g in range(1, 7):
            first = 3 * g + 1
            unit = divmod(TURNED[0] * CHUNK + g - 1, CHUNK)
            weigh_both_own(first)
            add_heads(nc.vector, late, None)
            for part in window_quantises.get(g, ()):
                finish(part)
            reduced = [(part, reduce_angles(part, *angles[part])) for part in window_reduces.get(g, ())]
            weigh_shared(first)
            add_heads(nc.gpsimd, first, None)
            transpose_halves(g, 0)
            weigh_own(first + 1, 0)
            make_some_values(1)
            weigh_own(first + 1, 1)
            weigh_shared(first + 1)
            add_heads(nc.gpsimd, first + 1, None)
            make_some_values(1)
            for part, behind in reduced:
                if part not in TURNED:
                    tables[part] = cosine_tables(part, behind)
            weigh_turned(*unit, 1)
            transpose_halves(g, 1)
            weigh_turned(*unit, 2)
            make_some_values(1)
            weigh_turned(*unit, 0)
            weigh_own(first + 2, 0)
            make_some_values(1)
            weigh_own(first + 2, 1)
            for part in window_reduces.get(g + 1, ()):
                angles[part] = lift_angles(part)
            weigh_shared(first + 2)
            late = first + 2
            make_some_values(1)
            for part, behind in reduced:
                if part in TURNED:
                    tables[part] = cosine_tables(part, behind)

        c = TURNED[1]
        weigh_both_own(LAST - 1)
        add_heads(nc.vector, late, None)
        weigh_shared(LAST - 1)
        add_heads(nc.gpsimd, LAST - 1, None)
        for n in (1, 2, 0):
            weigh_turned(c, 2, n)
        for half in range(2):
            turn_half(c, 1, half)
        store_turned(c, 1)
        for n in (1, 2, 0):
            weigh_turned(c, 3, n)
        weigh_both_own(LAST)
        weigh_shared(LAST)
        for half in range(2):
            turn_half(c, 2, half)
        store_turned(c, 2)
        add_heads(nc.vector, LAST, 0)
        add_heads(nc.vector, LAST, 1)
        for half in range(2):
            turn_half(c, 3, half)
        store_turned(c, 3)
